import numpy as np
import ml_dtypes


def mxq(x, axis, fmt="e4m3"):
    dtype, down = {"e4m3": (ml_dtypes.float8_e4m3fn, 7), "e5m2": (ml_dtypes.float8_e5m2, 14)}[fmt]
    v = np.moveaxis(np.asarray(x, np.float32).astype(ml_dtypes.bfloat16).astype(np.float64), axis, -1)
    blocks = v.reshape(v.shape[:-1] + (-1, 32))
    amax = np.abs(blocks).max(-1, keepdims=True)
    byte = np.maximum(np.where(amax > 0, np.frexp(amax)[1] - 1 + 127, 0) - down, 1)
    scale = np.exp2(byte - 127.0)
    codes = (blocks / scale).astype(np.float32).astype(dtype).astype(np.float64)
    return np.moveaxis((codes * scale).reshape(v.shape), -1, axis)


WIDE = False


def mx_kscale(k):
    if not WIDE:
        return np.ones(k)
    levels = np.array([20, -20, 10, -10, 0])
    a = np.random.permutation(np.resize(levels, k // 512 * 4)).reshape(k // 512, 4)
    idx = np.arange(k)
    return np.exp2(a[idx // 512, idx % 128 // 32])


BF16 = ml_dtypes.bfloat16


def bf(x):
    return np.asarray(x, np.float32).astype(BF16)


def f64(x):
    return np.asarray(x).astype(np.float64)


B, C, T, V, S = 4, 64, 16, 512, 4
O = C
K = S * V
N = O * B * T
EPS = 1e-5
ZS = 0.35
GS = 8.0


def aggregate(z, A):
    return np.moveaxis(f64(z), 0, 3).reshape(B, O, T, K) @ f64(A).reshape(K, V)


def norm_stats(y):
    mean = y.mean(axis=(0, 2, 3), keepdims=True)
    rstd = 1.0 / np.sqrt(y.var(axis=(0, 2, 3), keepdims=True) + EPS)
    return (y - mean) * rstd, rstd.reshape(O)


def setup_inputs():
    s = mx_kscale(N).reshape(O, B * T)[:, 0]
    z0 = bf((np.random.standard_normal((S, B, O, T, V)) + np.random.standard_normal(O)[None, None, :, None, None] / np.sqrt(K)) * ZS)
    A = bf(np.random.uniform(size=(S, V, V)))
    x = bf(np.random.standard_normal((B, C, T, V)))
    gamma = bf(1.0 + 0.1 * np.random.standard_normal(O))
    beta = bf(0.1 * np.random.standard_normal(O))
    g = bf(np.random.standard_normal((B, O, T, V)) * np.exp2(np.random.randint(-12, 1, (B, O, T, 1))) * GS / s[None, :, None, None])
    y_hat, rstd = norm_stats(aggregate(z0, A))
    return {"z": bf(f64(z0) * s[None, None, :, None, None]),
            "A": A,
            "x": x,
            "gamma": gamma,
            "beta": beta,
            "y_hat": np.asarray(y_hat, np.float32),
            "rstd": np.asarray(rstd, np.float32),
            "grad_out": g}


def reference(z, A, x, gamma, beta, y_hat, rstd, grad_out):
    yh = f64(y_hat)
    ga = f64(gamma)[None, :, None, None]
    be = f64(beta)[None, :, None, None]
    rs = f64(rstd)[None, :, None, None]
    pre = yh * ga + be + f64(x)
    dh = np.where(pre > 0.0, f64(grad_out), 0.0) * ga
    m1 = dh.mean(axis=(0, 2, 3), keepdims=True)
    m2 = (dh * yh).mean(axis=(0, 2, 3), keepdims=True)
    dy = rs * (dh - m1 - yh * m2)
    dn = np.transpose(dy, (1, 0, 2, 3)).reshape(N, V)
    zn = np.transpose(f64(z), (2, 1, 3, 0, 4)).reshape(N, K)
    da = mxq(zn, 0, "e4m3").T @ mxq(dn, 0, "e5m2")
    return da.reshape(S, V, V)

@@ -1,0 +1,291 @@
+import concourse.mybir as mybir
+from concourse.masks import make_identity
+
+F32 = mybir.dt.float32
+BF16 = mybir.dt.bfloat16
+U32 = mybir.dt.uint32
+U8 = mybir.dt.uint8
+E4M3_X4 = mybir.dt.float8_e4m3fn_x4
+E5M2_X4 = mybir.dt.float8_e5m2_x4
+ALU = mybir.AluOpType
+ACT = mybir.ActivationFunctionType
+AX = mybir.AxisListType
+
+S, B, O, T, V = 4, 4, 64, 16, 512
+P = 128
+PACK = 4
+PASSES = (O * B * T) // (P * PACK)
+CH = O // PASSES
+ROWS_PER_CH = P // CH
+ROW = PACK * V
+TILES = 2 * V // P
+COUNT = B * T * V
+HALF = PASSES // 2
+
+RAW_BUFS = 4
+GROUPED_A = 2
+GROUPED_B = 3
+
+FLOPS = 2 * (S * V) * V * (O * B * T)
+BYTES = 2 * S * B * O * T * V + (2 + 2 + 4) * B * O * T * V + 4 * S * V * V + 8 * O
+
+
+def load_pass(nc, dst, src):
+    for b in range(B):
+        nc.sync.dma_start(out=dst[b:P:B], in_=src[b])
+
+
+def regroup(copy, dst, src):
+    copy(
+        out=dst.rearrange("p (c i t) -> p c t i", i=4, t=PACK),
+        in_=src.rearrange("p (t c i) -> p c t i", i=4, t=PACK),
+    )
+
+
+def tile_dggcn_sparse_assemble_pa_v_kernel(tc, z, A, x, gamma, beta, y_hat, rstd, grad_out, out):
+    nc = tc.nc
+
+    x_v = x.rearrange("b (c ol) (tq j) w -> b c (ol tq) (j w)", ol=CH, j=PACK)
+    g_v = grad_out.rearrange("b (c ol) (tq j) w -> b c (ol tq) (j w)", ol=CH, j=PACK)
+    yh_v = y_hat.rearrange("b (c ol) (tq j) w -> b c (ol tq) (j w)", ol=CH, j=PACK)
+    z_v = z.rearrange("s b (c ol) (tq j) v -> b c (ol tq) s (j v)", ol=CH, j=PACK)
+
+    with tc.manual_schedule(), tc.tile_pool(name="consts", bufs=1) as consts, tc.tile_pool(
+        name="resident", bufs=1
+    ) as resident:
+        gamma_all = consts.tile([P, O], BF16, name="gamma_all")
+        beta_all = consts.tile([P, O], BF16, name="beta_all")
+        rstd_all = consts.tile([P, O], F32, name="rstd_all")
+        nc.scalar.dma_start(out=gamma_all[:], in_=gamma.partition_broadcast(P))
+        nc.scalar.dma_start(out=beta_all[:], in_=beta.partition_broadcast(P))
+        nc.scalar.dma_start(out=rstd_all[:], in_=rstd.partition_broadcast(P))
+
+        ident = consts.tile([P, P], F32, name="ident")
+        make_identity(nc, ident[:])
+        own_ch = consts.tile([P, CH], F32, name="own_ch")
+        nc.vector.tensor_reduce(
+            out=own_ch[:], in_=ident[:].rearrange("p (g i) -> p g i", i=ROWS_PER_CH), axis=AX.X, op=ALU.add
+        )
+        same_ch = consts.tile([P, P], F32, name="same_ch")
+        nc.vector.tensor_copy(
+            out=same_ch[:].rearrange("p (g i) -> p g i", i=ROWS_PER_CH),
+            in_=own_ch[:].unsqueeze(2).to_broadcast([P, CH, ROWS_PER_CH]),
+        )
+
+        def own_value(all_channels, name):
+            picked = consts.tile([P, PASSES, CH], F32, name=name + "_picked")
+            nc.vector.tensor_tensor(
+                out=picked[:],
+                in0=all_channels[:].rearrange("p (c ol) -> p c ol", ol=CH),
+                in1=own_ch[:].unsqueeze(1).to_broadcast([P, PASSES, CH]),
+                op=ALU.mult,
+            )
+            own = consts.tile([P, PASSES], F32, name=name)
+            nc.vector.tensor_reduce(out=own[:], in_=picked[:], axis=AX.X, op=ALU.add)
+            return own
+
+        ga = own_value(gamma_all, "ga")
+        be = own_value(beta_all, "be")
+        rs = own_value(rstd_all, "rs")
+        neg_be = consts.tile([P, PASSES], F32, name="neg_be")
+        nc.vector.tensor_scalar_mul(out=neg_be[:], in0=be[:], scalar1=-1.0)
+        rs_ga = consts.tile([P, PASSES], F32, name="rs_ga")
+        nc.vector.tensor_mul(out=rs_ga[:], in0=rs[:], in1=ga[:])
+
+        sums = consts.tile([P, 2, 2, HALF], F32, name="sums")
+        yh_factor = consts.tile([P, PASSES], F32, name="yh_factor")
+        offset = consts.tile([P, PASSES], F32, name="offset")
+
+        yh = [resident.tile([P, ROW], F32, name="yh%d" % c) for c in range(PASSES)]
+        mg = [resident.tile([P, ROW], BF16, name="mg%d" % c) for c in range(PASSES)]
+        z_codes = [resident.tile([P, 2 * V], U32, name="z_codes%d" % c, align_bytes=64) for c in range(PASSES)]
+        z_scales = [resident.tile([P, 2 * V], U8, name="z_scales%d" % c, align_bytes=64) for c in range(PASSES)]
+
+        def z_steps(s_pair, raw_pool, grouped_pool):
+            raw, grouped = {}, {}
+
+            def load(c):
+                raw[c] = raw_pool.tile([P, 2, ROW], BF16, name="z_raw")
+                load_pass(nc, raw[c], [z_v[b, c, :, 2 * s_pair : 2 * s_pair + 2, :] for b in range(B)])
+
+            def regroup_both(c, copies):
+                grouped[c] = grouped_pool.tile([P, 2, ROW], BF16, name="z_grouped", align_bytes=64)
+                for h in range(2):
+                    regroup(copies[h], grouped[c][:, h, :], raw[c][:, h, :])
+
+            def quantise(c):
+                nc.vector.quantize_mx(
+                    out=z_codes[c][:].bitcast(E4M3_X4),
+                    scales=z_scales[c][:],
+                    in_=grouped[c][:].rearrange("p h f -> p (h f)"),
+                )
+
+            return load, regroup_both, quantise
+
+        def scaled_y_hat(c):
+            col = slice(c, c + 1)
+            nc.scalar.activation(
+                out=yh[c][:], in_=yh[c][:], func=ACT.Identity, scale=yh_factor[:, col], bias=offset[:, col]
+            )
+
+        with tc.tile_pool(name="inputs", bufs=3) as inputs, tc.tile_pool(name="work", bufs=2) as works, tc.tile_pool(
+            name="raw_a", bufs=RAW_BUFS
+        ) as raw_a, tc.tile_pool(name="grouped_a", bufs=GROUPED_A) as grouped_a, tc.psum_pool(
+            name="stats", bufs=1
+        ) as stats:
+            load_z, regroup_z, quantise_z = z_steps(0, raw_a, grouped_a)
+            on_scalar = [nc.scalar.copy, nc.scalar.copy]
+            x_c, g_c, work = {}, {}, {}
+
+            def load_inputs(c):
+                load_pass(nc, yh[c], [yh_v[b, c] for b in range(B)])
+                x_c[c] = inputs.tile([P, ROW], BF16, name="x_c")
+                load_pass(nc, x_c[c], [x_v[b, c] for b in range(B)])
+                g_c[c] = inputs.tile([P, ROW], BF16, name="g_c")
+                load_pass(nc, g_c[c], [g_v[b, c] for b in range(B)])
+
+            def before_relu(c):
+                work[c] = works.tile([P, ROW], F32, name="work")
+                nc.vector.scalar_tensor_tensor(
+                    out=work[c][:], in0=yh[c][:], scalar=ga[:, c : c + 1], in1=x_c[c][:], op0=ALU.mult, op1=ALU.add
+                )
+
+            def masked_gradient(c):
+                nc.vector.scalar_tensor_tensor(
+                    out=mg[c][:],
+                    in0=work[c][:],
+                    scalar=neg_be[:, c : c + 1],
+                    in1=g_c[c][:],
+                    op0=ALU.is_gt,
+                    op1=ALU.mult,
+                    accum_out=sums[:, c // HALF, 0, c % HALF : c % HALF + 1],
+                )
+
+            def sum_with_y_hat(c):
+                nc.vector.scalar_tensor_tensor(
+                    out=work[c][:],
+                    in0=mg[c][:],
+                    scalar=1.0,
+                    in1=yh[c][:],
+                    op0=ALU.mult,
+                    op1=ALU.mult,
+                    accum_out=sums[:, c // HALF, 1, c % HALF : c % HALF + 1],
+                )
+
+            load_inputs(0)
+            load_z(0)
+            load_inputs(1)
+            load_z(1)
+            load_z(2)
+            regroup_z(0, on_scalar)
+            regroup_z(1, on_scalar)
+            before_relu(0)
+            for c in range(PASSES):
+                batch, last_of_batch = c // HALF, c % HALF == HALF - 1
+                if c + 2 < PASSES:
+                    load_inputs(c + 2)
+                if c + 3 < PASSES:
+                    load_z(c + 3)
+                masked_gradient(c)
+                if c + 1 < PASSES:
+                    before_relu(c + 1)
+                sum_with_y_hat(c)
+                if last_of_batch:
+                    totals = stats.tile([P, 2, HALF], F32, name="totals%d" % batch)
+                    nc.tensor.matmul(
+                        out=totals[:].rearrange("p k i -> p (k i)"),
+                        lhsT=same_ch[:],
+                        rhs=sums[:, batch].rearrange("p k i -> p (k i)"),
+                        start=True,
+                        stop=True,
+                    )
+                quantise_z(c)
+                if c + GROUPED_A < PASSES:
+                    regroup_z(c + GROUPED_A, on_scalar)
+                if last_of_batch:
+                    cols = slice(batch * HALF, (batch + 1) * HALF)
+                    for k, coefficient in enumerate([offset, yh_factor]):
+                        nc.vector.scalar_tensor_tensor(
+                            out=coefficient[:, cols],
+                            in0=totals[:, k, :],
+                            scalar=-1.0 / COUNT,
+                            in1=rs_ga[:, cols],
+                            op0=ALU.mult,
+                            op1=ALU.mult,
+                        )
+                if c >= HALF:
+                    scaled_y_hat(c - HALF)
+
+        with tc.tile_pool(name="dy_mx", bufs=1, reuse_waits="tile") as dy_mx, tc.tile_pool(
+            name="raw_b", bufs=RAW_BUFS, reuse_waits="tile"
+        ) as raw_b, tc.tile_pool(name="grouped_b", bufs=GROUPED_B, reuse_waits="tile") as grouped_b, tc.psum_pool(
+            name="acc", bufs=1
+        ) as accs:
+            dy_codes = [dy_mx.tile([P, V], U32, name="dy_codes%d" % c, align_bytes=64) for c in range(PASSES)]
+            dy_scales = [dy_mx.tile([P, V], U8, name="dy_scales%d" % c, align_bytes=64) for c in range(PASSES)]
+            load_z, regroup_z, quantise_z = z_steps(1, raw_b, grouped_b)
+
+            def multiply(acc, c):
+                for i in range(TILES):
+                    cols = slice(i * P, (i + 1) * P)
+                    nc.tensor.matmul_mx(
+                        out=acc[i][:],
+                        lhsT=z_codes[c][:, cols].bitcast(E4M3_X4),
+                        lhsT_scale=z_scales[c][:, cols],
+                        rhs=dy_codes[c][:].bitcast(E5M2_X4),
+                        rhs_scale=dy_scales[c][:],
+                        start=(c == 0),
+                        stop=(c == PASSES - 1),
+                    )
+
+            def store(results, acc, s_pair, copies):
+                for i in range(TILES):
+                    result = results.tile([P, V], F32, name="result")
+                    copies[i % 2](out=result[:], in_=acc[i][:])
+                    s, vt = 2 * s_pair + i * P // V, i % (V // P)
+                    nc.sync.dma_start(out=out[s, vt * P : (vt + 1) * P, :], in_=result[:])
+
+            for c in range(RAW_BUFS):
+                load_z(c)
+
+            acc = [accs.tile([P, V], F32, name="acc%d" % i) for i in range(TILES)]
+            with tc.tile_pool(name="dy_bf16", bufs=2, reuse_waits="tile") as dy_bf16:
+                dy_grouped = {}
+
+                def gradient_of_y(c):
+                    dy_grouped[c] = dy_bf16.tile([P, ROW], BF16, name="dy_grouped", align_bytes=64)
+                    nc.vector.scalar_tensor_tensor(
+                        out=dy_grouped[c][:].rearrange("p (w j) -> p w j", j=PACK),
+                        in0=mg[c][:].rearrange("p (j w) -> p w j", j=PACK),
+                        scalar=rs_ga[:, c : c + 1],
+                        in1=yh[c][:].rearrange("p (j w) -> p w j", j=PACK),
+                        op0=ALU.mult,
+                        op1=ALU.add,
+                    )
+
+                for c in range(HALF, PASSES):
+                    scaled_y_hat(c)
+                for c in range(GROUPED_B):
+                    regroup_z(c, [nc.scalar.copy, nc.scalar.copy])
+                    load_z(c + RAW_BUFS)
+                gradient_of_y(0)
+                for c in range(PASSES):
+                    if c + 1 < PASSES:
+                        gradient_of_y(c + 1)
+                    nc.vector.quantize_mx(
+                        out=dy_codes[c][:].bitcast(E5M2_X4), scales=dy_scales[c][:], in_=dy_grouped[c][:]
+                    )
+                    multiply(acc, c)
+
+            with tc.tile_pool(name="results", bufs=TILES, reuse_waits="tile") as results:
+                for c in range(PASSES):
+                    quantise_z(c)
+                    if c == 0:
+                        store(results, acc, 0, [nc.scalar.copy, nc.scalar.copy])
+                        acc = [accs.tile([P, V], F32, name="acc%d" % i) for i in range(TILES)]
+                    if c + GROUPED_B < PASSES:
+                        regroup_z(c + GROUPED_B, [nc.vector.tensor_copy, nc.scalar.copy])
+                        if c + GROUPED_B + RAW_BUFS < PASSES:
+                            load_z(c + GROUPED_B + RAW_BUFS)
+                    multiply(acc, c)
+                store(results, acc, 1, [nc.vector.tensor_copy, nc.scalar.copy])

@@ -20,7 +20,6 @@ ROWS_PER_CH = P // CH
 ROW = PACK * V
 TILES = 2 * V // P
 COUNT = B * T * V
-HALF = PASSES // 2
 
 RAW_BUFS = 4
 GROUPED_A = 2
@@ -92,9 +91,8 @@ def tile_dggcn_sparse_assemble_pa_v_kernel(tc, z, A, x, gamma, beta, y_hat, rstd
         rs_ga = consts.tile([P, PASSES], F32, name="rs_ga")
         nc.vector.tensor_mul(out=rs_ga[:], in0=rs[:], in1=ga[:])
 
-        sums = consts.tile([P, 2, 2, HALF], F32, name="sums")
-        yh_factor = consts.tile([P, PASSES], F32, name="yh_factor")
-        offset = consts.tile([P, PASSES], F32, name="offset")
+        sums = consts.tile([P, PASSES, 2], F32, name="sums")
+        line = consts.tile([P, PASSES, 2], F32, name="line")
 
         yh = [resident.tile([P, ROW], F32, name="yh%d" % c) for c in range(PASSES)]
         mg = [resident.tile([P, ROW], BF16, name="mg%d" % c) for c in range(PASSES)]
@@ -123,15 +121,14 @@ def tile_dggcn_sparse_assemble_pa_v_kernel(tc, z, A, x, gamma, beta, y_hat, rstd
             return load, regroup_both, quantise
 
         def scaled_y_hat(c):
-            col = slice(c, c + 1)
             nc.scalar.activation(
-                out=yh[c][:], in_=yh[c][:], func=ACT.Identity, scale=yh_factor[:, col], bias=offset[:, col]
+                out=yh[c][:], in_=yh[c][:], func=ACT.Identity, scale=line[:, c, 1:2], bias=line[:, c, 0:1]
             )
 
         with tc.tile_pool(name="inputs", bufs=3) as inputs, tc.tile_pool(name="work", bufs=2) as works, tc.tile_pool(
             name="raw_a", bufs=RAW_BUFS
         ) as raw_a, tc.tile_pool(name="grouped_a", bufs=GROUPED_A) as grouped_a, tc.psum_pool(
-            name="stats", bufs=1
+            name="stats", bufs=2
         ) as stats:
             load_z, regroup_z, quantise_z = z_steps(0, raw_a, grouped_a)
             on_scalar = [nc.scalar.copy, nc.scalar.copy]
@@ -158,7 +155,7 @@ def tile_dggcn_sparse_assemble_pa_v_kernel(tc, z, A, x, gamma, beta, y_hat, rstd
                     in1=g_c[c][:],
                     op0=ALU.is_gt,
                     op1=ALU.mult,
-                    accum_out=sums[:, c // HALF, 0, c % HALF : c % HALF + 1],
+                    accum_out=sums[:, c, 0:1],
                 )
 
             def sum_with_y_hat(c):
@@ -169,7 +166,7 @@ def tile_dggcn_sparse_assemble_pa_v_kernel(tc, z, A, x, gamma, beta, y_hat, rstd
                     in1=yh[c][:],
                     op0=ALU.mult,
                     op1=ALU.mult,
-                    accum_out=sums[:, c // HALF, 1, c % HALF : c % HALF + 1],
+                    accum_out=sums[:, c, 1:2],
                 )
 
             load_inputs(0)
@@ -181,7 +178,6 @@ def tile_dggcn_sparse_assemble_pa_v_kernel(tc, z, A, x, gamma, beta, y_hat, rstd
             regroup_z(1, on_scalar)
             before_relu(0)
             for c in range(PASSES):
-                batch, last_of_batch = c // HALF, c % HALF == HALF - 1
                 if c + 2 < PASSES:
                     load_inputs(c + 2)
                 if c + 3 < PASSES:
@@ -190,31 +186,20 @@ def tile_dggcn_sparse_assemble_pa_v_kernel(tc, z, A, x, gamma, beta, y_hat, rstd
                 if c + 1 < PASSES:
                     before_relu(c + 1)
                 sum_with_y_hat(c)
-                if last_of_batch:
-                    totals = stats.tile([P, 2, HALF], F32, name="totals%d" % batch)
-                    nc.tensor.matmul(
-                        out=totals[:].rearrange("p k i -> p (k i)"),
-                        lhsT=same_ch[:],
-                        rhs=sums[:, batch].rearrange("p k i -> p (k i)"),
-                        start=True,
-                        stop=True,
-                    )
+                totals = stats.tile([P, 2], F32, name="totals")
+                nc.tensor.matmul(out=totals[:], lhsT=same_ch[:], rhs=sums[:, c, :], start=True, stop=True)
                 quantise_z(c)
                 if c + GROUPED_A < PASSES:
                     regroup_z(c + GROUPED_A, on_scalar)
-                if last_of_batch:
-                    cols = slice(batch * HALF, (batch + 1) * HALF)
-                    for k, coefficient in enumerate([offset, yh_factor]):
-                        nc.vector.scalar_tensor_tensor(
-                            out=coefficient[:, cols],
-                            in0=totals[:, k, :],
-                            scalar=-1.0 / COUNT,
-                            in1=rs_ga[:, cols],
-                            op0=ALU.mult,
-                            op1=ALU.mult,
-                        )
-                if c >= HALF:
-                    scaled_y_hat(c - HALF)
+                nc.vector.tensor_scalar(
+                    out=line[:, c, :],
+                    in0=totals[:],
+                    scalar1=rs_ga[:, c : c + 1],
+                    scalar2=-1.0 / COUNT,
+                    op0=ALU.mult,
+                    op1=ALU.mult,
+                )
+                scaled_y_hat(c)
 
         with tc.tile_pool(name="dy_mx", bufs=1, reuse_waits="tile") as dy_mx, tc.tile_pool(
             name="raw_b", bufs=RAW_BUFS, reuse_waits="tile"
@@ -253,21 +238,13 @@ def tile_dggcn_sparse_assemble_pa_v_kernel(tc, z, A, x, gamma, beta, y_hat, rstd
                 dy_grouped = {}
 
                 def gradient_of_y(c):
-                    dy_grouped[c] = dy_bf16.tile([P, ROW], BF16, name="dy_grouped", align_bytes=64)
+                    dy_rows = dy_bf16.tile([P, ROW], BF16, name="dy_rows")
                     nc.vector.scalar_tensor_tensor(
-                        out=dy_grouped[c][:].rearrange("p (w j) -> p w j", j=PACK),
-                        in0=mg[c][:].rearrange("p (j w) -> p w j", j=PACK),
-                        scalar=rs_ga[:, c : c + 1],
-                        in1=yh[c][:].rearrange("p (j w) -> p w j", j=PACK),
-                        op0=ALU.mult,
-                        op1=ALU.add,
+                        out=dy_rows[:], in0=mg[c][:], scalar=rs_ga[:, c : c + 1], in1=yh[c][:], op0=ALU.mult, op1=ALU.add
                     )
+                    dy_grouped[c] = dy_bf16.tile([P, ROW], BF16, name="dy_grouped", align_bytes=64)
+                    regroup(nc.scalar.copy, dy_grouped[c][:], dy_rows[:])
 
-                for c in range(HALF, PASSES):
-                    scaled_y_hat(c)
-                for c in range(GROUPED_B):
-                    regroup_z(c, [nc.scalar.copy, nc.scalar.copy])
-                    load_z(c + RAW_BUFS)
                 gradient_of_y(0)
                 for c in range(PASSES):
                     if c + 1 < PASSES:
@@ -278,14 +255,17 @@ def tile_dggcn_sparse_assemble_pa_v_kernel(tc, z, A, x, gamma, beta, y_hat, rstd
                     multiply(acc, c)
 
             with tc.tile_pool(name="results", bufs=TILES, reuse_waits="tile") as results:
+                shared = [nc.vector.tensor_copy, nc.scalar.copy]
+                regroup_z(0, shared)
+                regroup_z(1, shared)
                 for c in range(PASSES):
                     quantise_z(c)
                     if c == 0:
-                        store(results, acc, 0, [nc.scalar.copy, nc.scalar.copy])
+                        store(results, acc, 0, shared)
                         acc = [accs.tile([P, V], F32, name="acc%d" % i) for i in range(TILES)]
-                    if c + GROUPED_B < PASSES:
-                        regroup_z(c + GROUPED_B, [nc.vector.tensor_copy, nc.scalar.copy])
-                        if c + GROUPED_B + RAW_BUFS < PASSES:
-                            load_z(c + GROUPED_B + RAW_BUFS)
+                    if c + 2 < PASSES:
+                        regroup_z(c + 2, shared)
+                    if c + RAW_BUFS < PASSES:
+                        load_z(c + RAW_BUFS)
                     multiply(acc, c)
-                store(results, acc, 1, [nc.vector.tensor_copy, nc.scalar.copy])
+                store(results, acc, 1, shared)

@@ -15,8 +15,9 @@ S, B, O, T, V = 4, 4, 64, 16, 512
 P = 128
 PACK = 4
 PASSES = (O * B * T) // (P * PACK)
-CH = O // PASSES
-ROWS_PER_CH = P // CH
+ROWS_PER_CH = 8
+CH = P // ROWS_PER_CH
+GROUPS = O // CH
 ROW = PACK * V
 TILES = 2 * V // P
 COUNT = B * T * V
@@ -30,8 +31,8 @@ BYTES = 2 * S * B * O * T * V + (2 + 2 + 4) * B * O * T * V + 4 * S * V * V + 8 
 
 
 def load_pass(nc, dst, src):
-    for b in range(B):
-        nc.sync.dma_start(out=dst[b:P:B], in_=src[b])
+    for bl in range(2):
+        nc.sync.dma_start(out=dst[bl:P:2], in_=src[bl])
 
 
 def regroup(copy, dst, src):
@@ -44,10 +45,11 @@ def regroup(copy, dst, src):
 def tile_dggcn_sparse_assemble_pa_v_kernel(tc, z, A, x, gamma, beta, y_hat, rstd, grad_out, out):
     nc = tc.nc
 
-    x_v = x.rearrange("b (c ol) (tq j) w -> b c (ol tq) (j w)", ol=CH, j=PACK)
-    g_v = grad_out.rearrange("b (c ol) (tq j) w -> b c (ol tq) (j w)", ol=CH, j=PACK)
-    yh_v = y_hat.rearrange("b (c ol) (tq j) w -> b c (ol tq) (j w)", ol=CH, j=PACK)
-    z_v = z.rearrange("s b (c ol) (tq j) v -> b c (ol tq) s (j v)", ol=CH, j=PACK)
+    rows = "(bh bl) (cg ol) (tq j) w -> cg bh bl (ol tq) (j w)"
+    x_v = x.rearrange(rows, bl=2, ol=CH, j=PACK)
+    g_v = grad_out.rearrange(rows, bl=2, ol=CH, j=PACK)
+    yh_v = y_hat.rearrange(rows, bl=2, ol=CH, j=PACK)
+    z_v = z.rearrange("s (bh bl) (cg ol) (tq j) v -> cg bh bl (ol tq) s (j v)", bl=2, ol=CH, j=PACK)
 
     with tc.manual_schedule(), tc.tile_pool(name="consts", bufs=1) as consts, tc.tile_pool(
         name="resident", bufs=1
@@ -72,27 +74,27 @@ def tile_dggcn_sparse_assemble_pa_v_kernel(tc, z, A, x, gamma, beta, y_hat, rstd
         )
 
         def own_value(all_channels, name):
-            picked = consts.tile([P, PASSES, CH], F32, name=name + "_picked")
+            picked = consts.tile([P, GROUPS, CH], F32, name=name + "_picked")
             nc.vector.tensor_tensor(
                 out=picked[:],
-                in0=all_channels[:].rearrange("p (c ol) -> p c ol", ol=CH),
-                in1=own_ch[:].unsqueeze(1).to_broadcast([P, PASSES, CH]),
+                in0=all_channels[:].rearrange("p (cg ol) -> p cg ol", ol=CH),
+                in1=own_ch[:].unsqueeze(1).to_broadcast([P, GROUPS, CH]),
                 op=ALU.mult,
             )
-            own = consts.tile([P, PASSES], F32, name=name)
+            own = consts.tile([P, GROUPS], F32, name=name)
             nc.vector.tensor_reduce(out=own[:], in_=picked[:], axis=AX.X, op=ALU.add)
             return own
 
         ga = own_value(gamma_all, "ga")
         be = own_value(beta_all, "be")
         rs = own_value(rstd_all, "rs")
-        neg_be = consts.tile([P, PASSES], F32, name="neg_be")
+        neg_be = consts.tile([P, GROUPS], F32, name="neg_be")
         nc.vector.tensor_scalar_mul(out=neg_be[:], in0=be[:], scalar1=-1.0)
-        rs_ga = consts.tile([P, PASSES], F32, name="rs_ga")
+        rs_ga = consts.tile([P, GROUPS], F32, name="rs_ga")
         nc.vector.tensor_mul(out=rs_ga[:], in0=rs[:], in1=ga[:])
 
         sums = consts.tile([P, PASSES, 2], F32, name="sums")
-        line = consts.tile([P, PASSES, 2], F32, name="line")
+        line = consts.tile([P, GROUPS, 2], F32, name="line")
 
         yh = [resident.tile([P, ROW], F32, name="yh%d" % c) for c in range(PASSES)]
         mg = [resident.tile([P, ROW], BF16, name="mg%d" % c) for c in range(PASSES)]
@@ -104,7 +106,7 @@ def tile_dggcn_sparse_assemble_pa_v_kernel(tc, z, A, x, gamma, beta, y_hat, rstd
 
             def load(c):
                 raw[c] = raw_pool.tile([P, 2, ROW], BF16, name="z_raw")
-                load_pass(nc, raw[c], [z_v[b, c, :, 2 * s_pair : 2 * s_pair + 2, :] for b in range(B)])
+                load_pass(nc, raw[c], z_v[c // 2, c % 2, :, :, 2 * s_pair : 2 * s_pair + 2, :])
 
             def regroup_both(c, copies):
                 grouped[c] = grouped_pool.tile([P, 2, ROW], BF16, name="z_grouped", align_bytes=64)
@@ -122,7 +124,7 @@ def tile_dggcn_sparse_assemble_pa_v_kernel(tc, z, A, x, gamma, beta, y_hat, rstd
 
         def scaled_y_hat(c):
             nc.scalar.activation(
-                out=yh[c][:], in_=yh[c][:], func=ACT.Identity, scale=line[:, c, 1:2], bias=line[:, c, 0:1]
+                out=yh[c][:], in_=yh[c][:], func=ACT.Identity, scale=line[:, c // 2, 1:2], bias=line[:, c // 2, 0:1]
             )
 
         with tc.tile_pool(name="inputs", bufs=3) as inputs, tc.tile_pool(name="work", bufs=2) as works, tc.tile_pool(
@@ -135,23 +137,23 @@ def tile_dggcn_sparse_assemble_pa_v_kernel(tc, z, A, x, gamma, beta, y_hat, rstd
             x_c, g_c, work = {}, {}, {}
 
             def load_inputs(c):
-                load_pass(nc, yh[c], [yh_v[b, c] for b in range(B)])
+                load_pass(nc, yh[c], yh_v[c // 2, c % 2])
                 x_c[c] = inputs.tile([P, ROW], BF16, name="x_c")
-                load_pass(nc, x_c[c], [x_v[b, c] for b in range(B)])
+                load_pass(nc, x_c[c], x_v[c // 2, c % 2])
                 g_c[c] = inputs.tile([P, ROW], BF16, name="g_c")
-                load_pass(nc, g_c[c], [g_v[b, c] for b in range(B)])
+                load_pass(nc, g_c[c], g_v[c // 2, c % 2])
 
             def before_relu(c):
                 work[c] = works.tile([P, ROW], F32, name="work")
                 nc.vector.scalar_tensor_tensor(
-                    out=work[c][:], in0=yh[c][:], scalar=ga[:, c : c + 1], in1=x_c[c][:], op0=ALU.mult, op1=ALU.add
+                    out=work[c][:], in0=yh[c][:], scalar=ga[:, c // 2 : c // 2 + 1], in1=x_c[c][:], op0=ALU.mult, op1=ALU.add
                 )
 
             def masked_gradient(c):
                 nc.vector.scalar_tensor_tensor(
                     out=mg[c][:],
                     in0=work[c][:],
-                    scalar=neg_be[:, c : c + 1],
+                    scalar=neg_be[:, c // 2 : c // 2 + 1],
                     in1=g_c[c][:],
                     op0=ALU.is_gt,
                     op1=ALU.mult,
@@ -178,6 +180,7 @@ def tile_dggcn_sparse_assemble_pa_v_kernel(tc, z, A, x, gamma, beta, y_hat, rstd
             regroup_z(1, on_scalar)
             before_relu(0)
             for c in range(PASSES):
+                cg, group_ends = c // 2, c % 2 == 1
                 if c + 2 < PASSES:
                     load_inputs(c + 2)
                 if c + 3 < PASSES:
@@ -186,20 +189,25 @@ def tile_dggcn_sparse_assemble_pa_v_kernel(tc, z, A, x, gamma, beta, y_hat, rstd
                 if c + 1 < PASSES:
                     before_relu(c + 1)
                 sum_with_y_hat(c)
-                totals = stats.tile([P, 2], F32, name="totals")
-                nc.tensor.matmul(out=totals[:], lhsT=same_ch[:], rhs=sums[:, c, :], start=True, stop=True)
+                if not group_ends:
+                    totals = stats.tile([P, 2], F32, name="totals")
+                nc.tensor.matmul(
+                    out=totals[:], lhsT=same_ch[:], rhs=sums[:, c, :], start=not group_ends, stop=group_ends
+                )
                 quantise_z(c)
                 if c + GROUPED_A < PASSES:
                     regroup_z(c + GROUPED_A, on_scalar)
-                nc.vector.tensor_scalar(
-                    out=line[:, c, :],
-                    in0=totals[:],
-                    scalar1=rs_ga[:, c : c + 1],
-                    scalar2=-1.0 / COUNT,
-                    op0=ALU.mult,
-                    op1=ALU.mult,
-                )
-                scaled_y_hat(c)
+                if group_ends:
+                    nc.vector.tensor_scalar(
+                        out=line[:, cg, :],
+                        in0=totals[:],
+                        scalar1=rs_ga[:, cg : cg + 1],
+                        scalar2=-1.0 / COUNT,
+                        op0=ALU.mult,
+                        op1=ALU.mult,
+                    )
+                if c >= 1:
+                    scaled_y_hat(c - 1)
 
         with tc.tile_pool(name="dy_mx", bufs=1, reuse_waits="tile") as dy_mx, tc.tile_pool(
             name="raw_b", bufs=RAW_BUFS, reuse_waits="tile"
@@ -238,13 +246,20 @@ def tile_dggcn_sparse_assemble_pa_v_kernel(tc, z, A, x, gamma, beta, y_hat, rstd
                 dy_grouped = {}
 
                 def gradient_of_y(c):
-                    dy_rows = dy_bf16.tile([P, ROW], BF16, name="dy_rows")
-                    nc.vector.scalar_tensor_tensor(
-                        out=dy_rows[:], in0=mg[c][:], scalar=rs_ga[:, c : c + 1], in1=yh[c][:], op0=ALU.mult, op1=ALU.add
-                    )
                     dy_grouped[c] = dy_bf16.tile([P, ROW], BF16, name="dy_grouped", align_bytes=64)
-                    regroup(nc.scalar.copy, dy_grouped[c][:], dy_rows[:])
+                    nc.vector.scalar_tensor_tensor(
+                        out=dy_grouped[c][:].rearrange("p (w j) -> p w j", j=PACK),
+                        in0=mg[c][:].rearrange("p (j w) -> p w j", j=PACK),
+                        scalar=rs_ga[:, c // 2 : c // 2 + 1],
+                        in1=yh[c][:].rearrange("p (j w) -> p w j", j=PACK),
+                        op0=ALU.mult,
+                        op1=ALU.add,
+                    )
 
+                scaled_y_hat(PASSES - 1)
+                for c in range(GROUPED_B):
+                    regroup_z(c, [nc.scalar.copy, nc.scalar.copy])
+                    load_z(c + RAW_BUFS)
                 gradient_of_y(0)
                 for c in range(PASSES):
                     if c + 1 < PASSES:
@@ -255,17 +270,14 @@ def tile_dggcn_sparse_assemble_pa_v_kernel(tc, z, A, x, gamma, beta, y_hat, rstd
                     multiply(acc, c)
 
             with tc.tile_pool(name="results", bufs=TILES, reuse_waits="tile") as results:
-                shared = [nc.vector.tensor_copy, nc.scalar.copy]
-                regroup_z(0, shared)
-                regroup_z(1, shared)
                 for c in range(PASSES):
                     quantise_z(c)
                     if c == 0:
-                        store(results, acc, 0, shared)
+                        store(results, acc, 0, [nc.scalar.copy, nc.scalar.copy])
                         acc = [accs.tile([P, V], F32, name="acc%d" % i) for i in range(TILES)]
-                    if c + 2 < PASSES:
-                        regroup_z(c + 2, shared)
-                    if c + RAW_BUFS < PASSES:
-                        load_z(c + RAW_BUFS)
+                    if c + GROUPED_B < PASSES:
+                        regroup_z(c + GROUPED_B, [nc.vector.tensor_copy, nc.scalar.copy])
+                        if c + GROUPED_B + RAW_BUFS < PASSES:
+                            load_z(c + GROUPED_B + RAW_BUFS)
                     multiply(acc, c)
-                store(results, acc, 1, shared)
+                store(results, acc, 1, [nc.vector.tensor_copy, nc.scalar.copy])

@@ -25,6 +25,9 @@ COUNT = B * T * V
 RAW_BUFS = 4
 GROUPED_A = 2
 GROUPED_B = 3
+BANK = 512
+CHUNKS = ROW // BANK
+ON_VECTOR = 2
 
 FLOPS = 2 * (S * V) * V * (O * B * T)
 BYTES = 2 * S * B * O * T * V + (2 + 2 + 4) * B * O * T * V + 4 * S * V * V + 8 * O
@@ -93,7 +96,14 @@ def tile_dggcn_sparse_assemble_pa_v_kernel(tc, z, A, x, gamma, beta, y_hat, rstd
         rs_ga = consts.tile([P, GROUPS], F32, name="rs_ga")
         nc.vector.tensor_mul(out=rs_ga[:], in0=rs[:], in1=ga[:])
 
-        sums = consts.tile([P, PASSES, 2], F32, name="sums")
+        sums = consts.tile([P, PASSES, CHUNKS, 2], F32, name="sums")
+        nc.vector.memset(sums[:], 0.0)
+        ident_bf = consts.tile([P, P], BF16, name="ident_bf")
+        nc.vector.tensor_copy(out=ident_bf[:], in_=ident[:])
+        diag_ga = [consts.tile([P, P], F32, name="diag_ga%d" % cg) for cg in range(GROUPS)]
+        for cg in range(GROUPS):
+            nc.vector.tensor_scalar_mul(out=diag_ga[cg][:], in0=ident[:], scalar1=ga[:, cg : cg + 1])
+        group_sums = consts.tile([P, GROUPS, 2], F32, name="group_sums")
         line = consts.tile([P, GROUPS, 2], F32, name="line")
 
         yh = [resident.tile([P, ROW], F32, name="yh%d" % c) for c in range(PASSES)]
@@ -131,10 +141,10 @@ def tile_dggcn_sparse_assemble_pa_v_kernel(tc, z, A, x, gamma, beta, y_hat, rstd
             name="raw_a", bufs=RAW_BUFS
         ) as raw_a, tc.tile_pool(name="grouped_a", bufs=GROUPED_A) as grouped_a, tc.psum_pool(
             name="stats", bufs=2
-        ) as stats:
+        ) as stats, tc.psum_pool(name="pres", bufs=6) as pres:
             load_z, regroup_z, quantise_z = z_steps(0, raw_a, grouped_a)
             on_scalar = [nc.scalar.copy, nc.scalar.copy]
-            x_c, g_c, work = {}, {}, {}
+            x_c, g_c, work, pre = {}, {}, {}, {}
 
             def load_inputs(c):
                 load_pass(nc, yh[c], yh_v[c // 2, c % 2])
@@ -149,16 +159,37 @@ def tile_dggcn_sparse_assemble_pa_v_kernel(tc, z, A, x, gamma, beta, y_hat, rstd
                     out=work[c][:], in0=yh[c][:], scalar=ga[:, c // 2 : c // 2 + 1], in1=x_c[c][:], op0=ALU.mult, op1=ALU.add
                 )
 
+            def before_relu_on_tensor(c):
+                for k in range(CHUNKS):
+                    cols = slice(k * BANK, (k + 1) * BANK)
+                    pre[c, k] = pres.tile([P, BANK], F32, name="pre")
+                    nc.tensor.matmul(out=pre[c, k][:], lhsT=diag_ga[c // 2][:], rhs=yh[c][:, cols], start=True, stop=False)
+                    nc.tensor.matmul(out=pre[c, k][:], lhsT=ident_bf[:], rhs=x_c[c][:, cols], start=False, stop=True)
+
             def masked_gradient(c):
-                nc.vector.scalar_tensor_tensor(
-                    out=mg[c][:],
-                    in0=work[c][:],
-                    scalar=neg_be[:, c // 2 : c // 2 + 1],
-                    in1=g_c[c][:],
-                    op0=ALU.is_gt,
-                    op1=ALU.mult,
-                    accum_out=sums[:, c, 0:1],
-                )
+                if c < ON_VECTOR:
+                    nc.vector.scalar_tensor_tensor(
+                        out=mg[c][:],
+                        in0=work[c][:],
+                        scalar=neg_be[:, c // 2 : c // 2 + 1],
+                        in1=g_c[c][:],
+                        op0=ALU.is_gt,
+                        op1=ALU.mult,
+                        accum_out=sums[:, c, 0, 0:1],
+                    )
+                    return
+                work[c] = works.tile([P, ROW], F32, name="work")
+                for k in range(CHUNKS):
+                    cols = slice(k * BANK, (k + 1) * BANK)
+                    nc.vector.scalar_tensor_tensor(
+                        out=mg[c][:, cols],
+                        in0=pre[c, k][:],
+                        scalar=neg_be[:, c // 2 : c // 2 + 1],
+                        in1=g_c[c][:, cols],
+                        op0=ALU.is_gt,
+                        op1=ALU.mult,
+                        accum_out=sums[:, c, k, 0:1],
+                    )
 
             def sum_with_y_hat(c):
                 nc.vector.scalar_tensor_tensor(
@@ -168,7 +199,7 @@ def tile_dggcn_sparse_assemble_pa_v_kernel(tc, z, A, x, gamma, beta, y_hat, rstd
                     in1=yh[c][:],
                     op0=ALU.mult,
                     op1=ALU.mult,
-                    accum_out=sums[:, c, 1:2],
+                    accum_out=sums[:, c, 0, 1:2],
                 )
 
             load_inputs(0)
@@ -186,21 +217,30 @@ def tile_dggcn_sparse_assemble_pa_v_kernel(tc, z, A, x, gamma, beta, y_hat, rstd
                 if c + 3 < PASSES:
                     load_z(c + 3)
                 masked_gradient(c)
-                if c + 1 < PASSES:
+                if c + 1 < ON_VECTOR:
                     before_relu(c + 1)
+                elif c + 1 < PASSES:
+                    before_relu_on_tensor(c + 1)
                 sum_with_y_hat(c)
                 if not group_ends:
-                    totals = stats.tile([P, 2], F32, name="totals")
+                    totals = stats.tile([P, CHUNKS, 2], F32, name="totals")
                 nc.tensor.matmul(
-                    out=totals[:], lhsT=same_ch[:], rhs=sums[:, c, :], start=not group_ends, stop=group_ends
+                    out=totals[:].rearrange("p k s -> p (k s)"),
+                    lhsT=same_ch[:],
+                    rhs=sums[:, c, :, :].rearrange("p k s -> p (k s)"),
+                    start=not group_ends,
+                    stop=group_ends,
                 )
                 quantise_z(c)
                 if c + GROUPED_A < PASSES:
                     regroup_z(c + GROUPED_A, on_scalar)
                 if group_ends:
+                    nc.vector.tensor_reduce(
+                        out=group_sums[:, cg, :], in_=totals[:].rearrange("p k s -> p s k"), axis=AX.X, op=ALU.add
+                    )
                     nc.vector.tensor_scalar(
                         out=line[:, cg, :],
-                        in0=totals[:],
+                        in0=group_sums[:, cg, :],
                         scalar1=rs_ga[:, cg : cg + 1],
                         scalar2=-1.0 / COUNT,
                         op0=ALU.mult,

@@ -21,13 +21,15 @@ GROUPS = O // CH
 ROW = PACK * V
 TILES = 2 * V // P
 COUNT = B * T * V
-
-RAW_BUFS = 4
-GROUPED_A = 2
-GROUPED_B = 3
 BANK = 512
 CHUNKS = ROW // BANK
-ON_VECTOR = 2
+Z_STEPS = 2 * PASSES
+
+PRE_BANKS = 6
+ON_VECTOR = (0, PASSES - 1)
+SHARED_FROM = 12
+RAW_BUFS = 4
+GROUPED_BUFS = 5
 
 FLOPS = 2 * (S * V) * V * (O * B * T)
 BYTES = 2 * S * B * O * T * V + (2 + 2 + 4) * B * O * T * V + 4 * S * V * V + 8 * O
@@ -38,11 +40,12 @@ def load_pass(nc, dst, src):
         nc.sync.dma_start(out=dst[bl:P:2], in_=src[bl])
 
 
-def regroup(copy, dst, src):
-    copy(
-        out=dst.rearrange("p (c i t) -> p c t i", i=4, t=PACK),
-        in_=src.rearrange("p (t c i) -> p c t i", i=4, t=PACK),
-    )
+def grouped_view(ap):
+    return ap.rearrange("p (c i t) -> p c t i", i=4, t=PACK)
+
+
+def rows_view(ap):
+    return ap.rearrange("p (t c i) -> p c t i", i=4, t=PACK)
 
 
 def tile_dggcn_sparse_assemble_pa_v_kernel(tc, z, A, x, gamma, beta, y_hat, rstd, grad_out, out):
@@ -55,8 +58,12 @@ def tile_dggcn_sparse_assemble_pa_v_kernel(tc, z, A, x, gamma, beta, y_hat, rstd
     z_v = z.rearrange("s (bh bl) (cg ol) (tq j) v -> cg bh bl (ol tq) s (j v)", bl=2, ol=CH, j=PACK)
 
     with tc.manual_schedule(), tc.tile_pool(name="consts", bufs=1) as consts, tc.tile_pool(
-        name="resident", bufs=1
-    ) as resident:
+        name="codes", bufs=1
+    ) as codes, tc.tile_pool(name="yhs", bufs=5) as yhs, tc.tile_pool(name="mgs", bufs=3) as mgs, tc.tile_pool(
+        name="inputs", bufs=3
+    ) as inputs, tc.tile_pool(name="works", bufs=1) as works, tc.tile_pool(name="raws", bufs=RAW_BUFS) as raws, tc.tile_pool(
+        name="groupeds", bufs=GROUPED_BUFS
+    ) as groupeds, tc.tile_pool(name="dygs", bufs=2) as dygs, tc.psum_pool(name="banks", bufs=1) as banks:
         gamma_all = consts.tile([P, O], BF16, name="gamma_all")
         beta_all = consts.tile([P, O], BF16, name="beta_all")
         rstd_all = consts.tile([P, O], F32, name="rstd_all")
@@ -66,14 +73,17 @@ def tile_dggcn_sparse_assemble_pa_v_kernel(tc, z, A, x, gamma, beta, y_hat, rstd
 
         ident = consts.tile([P, P], F32, name="ident")
         make_identity(nc, ident[:])
+        ident_bf = consts.tile([P, P], BF16, name="ident_bf")
+        nc.vector.tensor_copy(out=ident_bf[:], in_=ident[:])
         own_ch = consts.tile([P, CH], F32, name="own_ch")
         nc.vector.tensor_reduce(
             out=own_ch[:], in_=ident[:].rearrange("p (g i) -> p g i", i=ROWS_PER_CH), axis=AX.X, op=ALU.add
         )
-        same_ch = consts.tile([P, P], F32, name="same_ch")
-        nc.vector.tensor_copy(
-            out=same_ch[:].rearrange("p (g i) -> p g i", i=ROWS_PER_CH),
-            in_=own_ch[:].unsqueeze(2).to_broadcast([P, CH, ROWS_PER_CH]),
+        minus_mean = consts.tile([P, P], F32, name="minus_mean")
+        nc.vector.tensor_scalar_mul(
+            out=minus_mean[:].rearrange("p (g i) -> p g i", i=ROWS_PER_CH),
+            in0=own_ch[:].unsqueeze(2).to_broadcast([P, CH, ROWS_PER_CH]),
+            scalar1=-1.0 / COUNT,
         )
 
         def own_value(all_channels, name):
@@ -95,229 +105,240 @@ def tile_dggcn_sparse_assemble_pa_v_kernel(tc, z, A, x, gamma, beta, y_hat, rstd
         nc.vector.tensor_scalar_mul(out=neg_be[:], in0=be[:], scalar1=-1.0)
         rs_ga = consts.tile([P, GROUPS], F32, name="rs_ga")
         nc.vector.tensor_mul(out=rs_ga[:], in0=rs[:], in1=ga[:])
-
-        sums = consts.tile([P, PASSES, CHUNKS, 2], F32, name="sums")
-        nc.vector.memset(sums[:], 0.0)
-        ident_bf = consts.tile([P, P], BF16, name="ident_bf")
-        nc.vector.tensor_copy(out=ident_bf[:], in_=ident[:])
         diag_ga = [consts.tile([P, P], F32, name="diag_ga%d" % cg) for cg in range(GROUPS)]
         for cg in range(GROUPS):
             nc.vector.tensor_scalar_mul(out=diag_ga[cg][:], in0=ident[:], scalar1=ga[:, cg : cg + 1])
-        group_sums = consts.tile([P, GROUPS, 2], F32, name="group_sums")
-        line = consts.tile([P, GROUPS, 2], F32, name="line")
 
-        yh = [resident.tile([P, ROW], F32, name="yh%d" % c) for c in range(PASSES)]
-        mg = [resident.tile([P, ROW], BF16, name="mg%d" % c) for c in range(PASSES)]
-        z_codes = [resident.tile([P, 2 * V], U32, name="z_codes%d" % c, align_bytes=64) for c in range(PASSES)]
-        z_scales = [resident.tile([P, 2 * V], U8, name="z_scales%d" % c, align_bytes=64) for c in range(PASSES)]
+        sums = consts.tile([P, PASSES, CHUNKS, 2], F32, name="sums")
+        nc.vector.memset(sums[:], 0.0)
+        coef = consts.tile([P, GROUPS, 2], F32, name="coef")
+        shift = consts.tile([P, GROUPS], F32, name="shift")
 
-        def z_steps(s_pair, raw_pool, grouped_pool):
-            raw, grouped = {}, {}
+        z_codes = [codes.tile([P, 2 * V], U32, name="z_codes%d" % c, align_bytes=64) for c in range(PASSES)]
+        z_scales = [codes.tile([P, 2 * V], U8, name="z_scales%d" % c, align_bytes=64) for c in range(PASSES)]
+        dy_codes = [codes.tile([P, V], U32, name="dy_codes%d" % c, align_bytes=64) for c in range(PASSES)]
+        dy_scales = [codes.tile([P, V], U8, name="dy_scales%d" % c, align_bytes=64) for c in range(PASSES)]
 
-            def load(c):
-                raw[c] = raw_pool.tile([P, 2, ROW], BF16, name="z_raw")
-                load_pass(nc, raw[c], z_v[c // 2, c % 2, :, :, 2 * s_pair : 2 * s_pair + 2, :])
+        yh, x_c, g_c, mg, work, pre, raw, grouped, dyg = {}, {}, {}, {}, {}, {}, {}, {}, {}
 
-            def regroup_both(c, copies):
-                grouped[c] = grouped_pool.tile([P, 2, ROW], BF16, name="z_grouped", align_bytes=64)
-                for h in range(2):
-                    regroup(copies[h], grouped[c][:, h, :], raw[c][:, h, :])
+        def bank(b, shape):
+            return banks.tile(shape, F32, name="bank%d" % b)
 
-            def quantise(c):
-                nc.vector.quantize_mx(
-                    out=z_codes[c][:].bitcast(E4M3_X4),
-                    scales=z_scales[c][:],
-                    in_=grouped[c][:].rearrange("p h f -> p (h f)"),
-                )
+        def load_inputs(c):
+            yh[c] = yhs.tile([P, ROW], F32, name="yh")
+            load_pass(nc, yh[c], yh_v[c // 2, c % 2])
+            x_c[c] = inputs.tile([P, ROW], BF16, name="x_c")
+            load_pass(nc, x_c[c], x_v[c // 2, c % 2])
+            g_c[c] = inputs.tile([P, ROW], BF16, name="g_c")
+            load_pass(nc, g_c[c], g_v[c // 2, c % 2])
 
-            return load, regroup_both, quantise
+        def load_z(zi):
+            s_pair, c = divmod(zi, PASSES)
+            raw[zi] = raws.tile([P, 2, ROW], BF16, name="z_raw")
+            load_pass(nc, raw[zi], z_v[c // 2, c % 2, :, :, 2 * s_pair : 2 * s_pair + 2, :])
 
-        def scaled_y_hat(c):
-            nc.scalar.activation(
-                out=yh[c][:], in_=yh[c][:], func=ACT.Identity, scale=line[:, c // 2, 1:2], bias=line[:, c // 2, 0:1]
+        def regroup_z(half):
+            zi, h = divmod(half, 2)
+            if h == 0:
+                grouped[zi] = groupeds.tile([P, 2, ROW], BF16, name="z_grouped", align_bytes=64)
+            copy = nc.vector.tensor_copy if zi >= SHARED_FROM and h == 0 else nc.scalar.copy
+            copy(out=grouped_view(grouped[zi][:, h, :]), in_=rows_view(raw[zi][:, h, :]))
+
+        def quantise_z(zi):
+            nc.vector.quantize_mx(
+                out=z_codes[zi % PASSES][:].bitcast(E4M3_X4),
+                scales=z_scales[zi % PASSES][:],
+                in_=grouped[zi][:].rearrange("p h f -> p (h f)"),
             )
 
-        with tc.tile_pool(name="inputs", bufs=3) as inputs, tc.tile_pool(name="work", bufs=2) as works, tc.tile_pool(
-            name="raw_a", bufs=RAW_BUFS
-        ) as raw_a, tc.tile_pool(name="grouped_a", bufs=GROUPED_A) as grouped_a, tc.psum_pool(
-            name="stats", bufs=2
-        ) as stats, tc.psum_pool(name="pres", bufs=6) as pres:
-            load_z, regroup_z, quantise_z = z_steps(0, raw_a, grouped_a)
-            on_scalar = [nc.scalar.copy, nc.scalar.copy]
-            x_c, g_c, work, pre = {}, {}, {}, {}
+        def before_relu(c):
+            work[c] = works.tile([P, ROW], F32, name="work")
+            nc.vector.scalar_tensor_tensor(
+                out=work[c][:], in0=yh[c][:], scalar=ga[:, c // 2 : c // 2 + 1], in1=x_c[c][:], op0=ALU.mult, op1=ALU.add
+            )
 
-            def load_inputs(c):
-                load_pass(nc, yh[c], yh_v[c // 2, c % 2])
-                x_c[c] = inputs.tile([P, ROW], BF16, name="x_c")
-                load_pass(nc, x_c[c], x_v[c // 2, c % 2])
-                g_c[c] = inputs.tile([P, ROW], BF16, name="g_c")
-                load_pass(nc, g_c[c], g_v[c // 2, c % 2])
+        def before_relu_on_tensor(c):
+            for k in range(CHUNKS):
+                cols = slice(k * BANK, (k + 1) * BANK)
+                pre[c, k] = bank((CHUNKS * (c - 1) + k) % PRE_BANKS, [P, BANK])
+                nc.tensor.matmul(out=pre[c, k][:], lhsT=diag_ga[c // 2][:], rhs=yh[c][:, cols], start=True, stop=False)
+                nc.tensor.matmul(out=pre[c, k][:], lhsT=ident_bf[:], rhs=x_c[c][:, cols], start=False, stop=True)
 
-            def before_relu(c):
-                work[c] = works.tile([P, ROW], F32, name="work")
+        def masked_gradient(c):
+            mg[c] = mgs.tile([P, ROW], BF16, name="mg")
+            pieces = [(0, slice(0, ROW), work[c])] if c in ON_VECTOR else [
+                (k, slice(k * BANK, (k + 1) * BANK), pre[c, k]) for k in range(CHUNKS)
+            ]
+            for k, cols, before in pieces:
                 nc.vector.scalar_tensor_tensor(
-                    out=work[c][:], in0=yh[c][:], scalar=ga[:, c // 2 : c // 2 + 1], in1=x_c[c][:], op0=ALU.mult, op1=ALU.add
-                )
-
-            def before_relu_on_tensor(c):
-                for k in range(CHUNKS):
-                    cols = slice(k * BANK, (k + 1) * BANK)
-                    pre[c, k] = pres.tile([P, BANK], F32, name="pre")
-                    nc.tensor.matmul(out=pre[c, k][:], lhsT=diag_ga[c // 2][:], rhs=yh[c][:, cols], start=True, stop=False)
-                    nc.tensor.matmul(out=pre[c, k][:], lhsT=ident_bf[:], rhs=x_c[c][:, cols], start=False, stop=True)
-
-            def masked_gradient(c):
-                if c < ON_VECTOR:
-                    nc.vector.scalar_tensor_tensor(
-                        out=mg[c][:],
-                        in0=work[c][:],
-                        scalar=neg_be[:, c // 2 : c // 2 + 1],
-                        in1=g_c[c][:],
-                        op0=ALU.is_gt,
-                        op1=ALU.mult,
-                        accum_out=sums[:, c, 0, 0:1],
-                    )
-                    return
-                work[c] = works.tile([P, ROW], F32, name="work")
-                for k in range(CHUNKS):
-                    cols = slice(k * BANK, (k + 1) * BANK)
-                    nc.vector.scalar_tensor_tensor(
-                        out=mg[c][:, cols],
-                        in0=pre[c, k][:],
-                        scalar=neg_be[:, c // 2 : c // 2 + 1],
-                        in1=g_c[c][:, cols],
-                        op0=ALU.is_gt,
-                        op1=ALU.mult,
-                        accum_out=sums[:, c, k, 0:1],
-                    )
-
-            def sum_with_y_hat(c):
-                nc.vector.scalar_tensor_tensor(
-                    out=work[c][:],
-                    in0=mg[c][:],
-                    scalar=1.0,
-                    in1=yh[c][:],
-                    op0=ALU.mult,
+                    out=mg[c][:, cols],
+                    in0=before[:],
+                    scalar=neg_be[:, c // 2 : c // 2 + 1],
+                    in1=g_c[c][:, cols],
+                    op0=ALU.is_gt,
                     op1=ALU.mult,
-                    accum_out=sums[:, c, 0, 1:2],
+                    accum_out=sums[:, c, k, 0:1],
                 )
 
-            load_inputs(0)
-            load_z(0)
-            load_inputs(1)
-            load_z(1)
-            load_z(2)
-            regroup_z(0, on_scalar)
-            regroup_z(1, on_scalar)
-            before_relu(0)
-            for c in range(PASSES):
-                cg, group_ends = c // 2, c % 2 == 1
-                if c + 2 < PASSES:
-                    load_inputs(c + 2)
-                if c + 3 < PASSES:
-                    load_z(c + 3)
-                masked_gradient(c)
-                if c + 1 < ON_VECTOR:
-                    before_relu(c + 1)
-                elif c + 1 < PASSES:
-                    before_relu_on_tensor(c + 1)
-                sum_with_y_hat(c)
-                if not group_ends:
-                    totals = stats.tile([P, CHUNKS, 2], F32, name="totals")
-                nc.tensor.matmul(
-                    out=totals[:].rearrange("p k s -> p (k s)"),
-                    lhsT=same_ch[:],
-                    rhs=sums[:, c, :, :].rearrange("p k s -> p (k s)"),
-                    start=not group_ends,
-                    stop=group_ends,
+        def sum_with_y_hat(c):
+            if c not in ON_VECTOR:
+                work[c] = works.tile([P, ROW], F32, name="work")
+            nc.vector.scalar_tensor_tensor(
+                out=work[c][:],
+                in0=mg[c][:],
+                scalar=1.0,
+                in1=yh[c][:],
+                op0=ALU.mult,
+                op1=ALU.mult,
+                accum_out=sums[:, c, 0, 1:2],
+            )
+
+        def add_up(c, totals):
+            nc.tensor.matmul(
+                out=totals[:].rearrange("p k s -> p (k s)"),
+                lhsT=minus_mean[:],
+                rhs=sums[:, c, :, :].rearrange("p k s -> p (k s)"),
+                start=(c % 2 == 0),
+                stop=(c % 2 == 1),
+            )
+
+        def coefficients(cg, totals):
+            nc.vector.tensor_reduce(out=coef[:, cg, :], in_=totals[:].rearrange("p k s -> p s k"), axis=AX.X, op=ALU.add)
+            nc.vector.tensor_mul(out=shift[:, cg : cg + 1], in0=coef[:, cg, 0:1], in1=rs_ga[:, cg : cg + 1])
+
+        def centre(c):
+            nc.vector.scalar_tensor_tensor(
+                out=yh[c][:], in0=yh[c][:], scalar=coef[:, c // 2, 1:2], in1=mg[c][:], op0=ALU.mult, op1=ALU.add
+            )
+
+        def finish(c):
+            dyg[c] = dygs.tile([P, ROW], BF16, name="dy_grouped", align_bytes=64)
+            nc.scalar.activation(
+                out=grouped_view(dyg[c][:]),
+                in_=rows_view(yh[c][:]),
+                func=ACT.Identity,
+                scale=rs_ga[:, c // 2 : c // 2 + 1],
+                bias=shift[:, c // 2 : c // 2 + 1],
+            )
+
+        def quantise_dy(c):
+            nc.vector.quantize_mx(out=dy_codes[c][:].bitcast(E5M2_X4), scales=dy_scales[c][:], in_=dyg[c][:])
+
+        def multiply(acc, c, tiles):
+            for i in tiles:
+                cols = slice(i * P, (i + 1) * P)
+                nc.tensor.matmul_mx(
+                    out=acc[i][:],
+                    lhsT=z_codes[c][:, cols].bitcast(E4M3_X4),
+                    lhsT_scale=z_scales[c][:, cols],
+                    rhs=dy_codes[c][:].bitcast(E5M2_X4),
+                    rhs_scale=dy_scales[c][:],
+                    start=(c == 0),
+                    stop=(c == PASSES - 1),
                 )
-                quantise_z(c)
-                if c + GROUPED_A < PASSES:
-                    regroup_z(c + GROUPED_A, on_scalar)
-                if group_ends:
-                    nc.vector.tensor_reduce(
-                        out=group_sums[:, cg, :], in_=totals[:].rearrange("p k s -> p s k"), axis=AX.X, op=ALU.add
-                    )
-                    nc.vector.tensor_scalar(
-                        out=line[:, cg, :],
-                        in0=group_sums[:, cg, :],
-                        scalar1=rs_ga[:, cg : cg + 1],
-                        scalar2=-1.0 / COUNT,
-                        op0=ALU.mult,
-                        op1=ALU.mult,
-                    )
-                if c >= 1:
-                    scaled_y_hat(c - 1)
 
-        with tc.tile_pool(name="dy_mx", bufs=1, reuse_waits="tile") as dy_mx, tc.tile_pool(
-            name="raw_b", bufs=RAW_BUFS, reuse_waits="tile"
-        ) as raw_b, tc.tile_pool(name="grouped_b", bufs=GROUPED_B, reuse_waits="tile") as grouped_b, tc.psum_pool(
-            name="acc", bufs=1
-        ) as accs:
-            dy_codes = [dy_mx.tile([P, V], U32, name="dy_codes%d" % c, align_bytes=64) for c in range(PASSES)]
-            dy_scales = [dy_mx.tile([P, V], U8, name="dy_scales%d" % c, align_bytes=64) for c in range(PASSES)]
-            load_z, regroup_z, quantise_z = z_steps(1, raw_b, grouped_b)
+        idle = [(inputs, "x_c"), (inputs, "g_c"), (mgs, "mg")]
+        result = {}
 
-            def multiply(acc, c):
+        def empty(acc, i):
+            pool, name = idle[i % len(idle)]
+            result[i] = pool.tile([P, V], F32, name=name)
+            (nc.vector.tensor_copy, nc.scalar.copy)[i % 2](out=result[i][:], in_=acc[i][:])
+
+        def store(s_pair, i):
+            s, vt = 2 * s_pair + i * P // V, i % (V // P)
+            nc.sync.dma_start(out=out[s, vt * P : (vt + 1) * P, :], in_=result[i][:])
+
+        state = {"loaded": 0, "halves": 0}
+
+        def load_z_up_to(last):
+            while state["loaded"] <= min(last, Z_STEPS - 1, state["halves"] // 2 + RAW_BUFS - 1):
+                load_z(state["loaded"])
+                state["loaded"] += 1
+
+        def regroup_up_to(halves):
+            while state["halves"] < min(halves, 2 * state["loaded"]):
+                regroup_z(state["halves"])
+                state["halves"] += 1
+
+        load_inputs(0)
+        load_inputs(1)
+        load_z_up_to(0)
+        before_relu(0)
+        acc, totals = {}, None
+        for c in range(PASSES):
+            halves = 2 * (c + 2) + min(max(0, c - 2), 4)
+            if c + 2 < PASSES:
+                load_inputs(c + 2)
+            load_z_up_to((halves - 1) // 2 + min(c, 1))
+            masked_gradient(c)
+            if c + 1 < PASSES and c + 1 not in ON_VECTOR:
+                before_relu_on_tensor(c + 1)
+            sum_with_y_hat(c)
+            if c + 1 in ON_VECTOR:
+                before_relu(c + 1)
+            if c % 2 == 0:
+                totals = bank(PRE_BANKS + (c // 2) % 2, [P, CHUNKS, 2])
+            add_up(c, totals)
+            if c >= 1:
+                quantise_z(c - 1)
+            regroup_up_to(2 * (c + 2))
+            if c >= 2:
+                centre(c - 2)
+                finish(c - 2)
+            if c < PASSES - 1:
+                regroup_up_to(halves)
+            if c >= 3:
+                quantise_dy(c - 3)
+            if c % 2 == 1:
+                coefficients(c // 2, totals)
+            if c == PASSES - 2:
+                for i in range(TILES - 1):
+                    acc[i] = bank(i, [P, V])
+                for done in range(c - 2):
+                    multiply(acc, done, range(TILES - 1))
+            if c == PASSES - 1:
+                acc[TILES - 1] = bank(TILES - 1, [P, V])
+                for done in range(c - 3):
+                    multiply(acc, done, [TILES - 1])
+                multiply(acc, c - 3, range(TILES))
+
+        centre(PASSES - 2)
+        finish(PASSES - 2)
+        quantise_dy(PASSES - 3)
+        multiply(acc, PASSES - 3, range(TILES))
+        centre(PASSES - 1)
+        finish(PASSES - 1)
+        quantise_z(PASSES - 1)
+        quantise_dy(PASSES - 2)
+        multiply(acc, PASSES - 2, range(TILES))
+        load_z_up_to(Z_STEPS - 1)
+        regroup_up_to(state["halves"] + 1)
+        quantise_z(PASSES)
+        quantise_dy(PASSES - 1)
+        multiply(acc, PASSES - 1, range(TILES))
+        quantise_z(PASSES + 1)
+        for i in range(TILES):
+            empty(acc, i)
+        regroup_up_to(2 * SHARED_FROM)
+        load_z_up_to(Z_STEPS - 1)
+        for i in range(TILES):
+            acc[i] = bank(i, [P, V])
+        multiply(acc, 0, range(TILES))
+        multiply(acc, 1, range(TILES))
+        stored = False
+        for zi in range(PASSES + 2, Z_STEPS):
+            regroup_up_to(2 * (zi + 1))
+            load_z_up_to(Z_STEPS - 1)
+            if state["loaded"] == Z_STEPS and not stored:
                 for i in range(TILES):
-                    cols = slice(i * P, (i + 1) * P)
-                    nc.tensor.matmul_mx(
-                        out=acc[i][:],
-                        lhsT=z_codes[c][:, cols].bitcast(E4M3_X4),
-                        lhsT_scale=z_scales[c][:, cols],
-                        rhs=dy_codes[c][:].bitcast(E5M2_X4),
-                        rhs_scale=dy_scales[c][:],
-                        start=(c == 0),
-                        stop=(c == PASSES - 1),
-                    )
-
-            def store(results, acc, s_pair, copies):
-                for i in range(TILES):
-                    result = results.tile([P, V], F32, name="result")
-                    copies[i % 2](out=result[:], in_=acc[i][:])
-                    s, vt = 2 * s_pair + i * P // V, i % (V // P)
-                    nc.sync.dma_start(out=out[s, vt * P : (vt + 1) * P, :], in_=result[:])
-
-            for c in range(RAW_BUFS):
-                load_z(c)
-
-            acc = [accs.tile([P, V], F32, name="acc%d" % i) for i in range(TILES)]
-            with tc.tile_pool(name="dy_bf16", bufs=2, reuse_waits="tile") as dy_bf16:
-                dy_grouped = {}
-
-                def gradient_of_y(c):
-                    dy_grouped[c] = dy_bf16.tile([P, ROW], BF16, name="dy_grouped", align_bytes=64)
-                    nc.vector.scalar_tensor_tensor(
-                        out=dy_grouped[c][:].rearrange("p (w j) -> p w j", j=PACK),
-                        in0=mg[c][:].rearrange("p (j w) -> p w j", j=PACK),
-                        scalar=rs_ga[:, c // 2 : c // 2 + 1],
-                        in1=yh[c][:].rearrange("p (j w) -> p w j", j=PACK),
-                        op0=ALU.mult,
-                        op1=ALU.add,
-                    )
-
-                scaled_y_hat(PASSES - 1)
-                for c in range(GROUPED_B):
-                    regroup_z(c, [nc.scalar.copy, nc.scalar.copy])
-                    load_z(c + RAW_BUFS)
-                gradient_of_y(0)
-                for c in range(PASSES):
-                    if c + 1 < PASSES:
-                        gradient_of_y(c + 1)
-                    nc.vector.quantize_mx(
-                        out=dy_codes[c][:].bitcast(E5M2_X4), scales=dy_scales[c][:], in_=dy_grouped[c][:]
-                    )
-                    multiply(acc, c)
-
-            with tc.tile_pool(name="results", bufs=TILES, reuse_waits="tile") as results:
-                for c in range(PASSES):
-                    quantise_z(c)
-                    if c == 0:
-                        store(results, acc, 0, [nc.scalar.copy, nc.scalar.copy])
-                        acc = [accs.tile([P, V], F32, name="acc%d" % i) for i in range(TILES)]
-                    if c + GROUPED_B < PASSES:
-                        regroup_z(c + GROUPED_B, [nc.vector.tensor_copy, nc.scalar.copy])
-                        if c + GROUPED_B + RAW_BUFS < PASSES:
-                            load_z(c + GROUPED_B + RAW_BUFS)
-                    multiply(acc, c)
-                store(results, acc, 1, [nc.vector.tensor_copy, nc.scalar.copy])
+                    store(0, i)
+                stored = True
+            quantise_z(zi)
+            if zi < Z_STEPS - 2:
+                multiply(acc, zi - PASSES, range(TILES))
+        for i in range(TILES):
+            multiply(acc, PASSES - 2, [i])
+            multiply(acc, PASSES - 1, [i])
+            empty(acc, i)
+            store(1, i)

@@ -64,12 +64,21 @@ def tile_dggcn_sparse_assemble_pa_v_kernel(tc, z, A, x, gamma, beta, y_hat, rstd
     ) as inputs, tc.tile_pool(name="works", bufs=1) as works, tc.tile_pool(name="raws", bufs=RAW_BUFS) as raws, tc.tile_pool(
         name="groupeds", bufs=GROUPED_BUFS
     ) as groupeds, tc.tile_pool(name="dygs", bufs=2) as dygs, tc.psum_pool(name="banks", bufs=1) as banks:
-        gamma_all = consts.tile([P, O], BF16, name="gamma_all")
-        beta_all = consts.tile([P, O], BF16, name="beta_all")
-        rstd_all = consts.tile([P, O], F32, name="rstd_all")
-        nc.scalar.dma_start(out=gamma_all[:], in_=gamma.partition_broadcast(P))
-        nc.scalar.dma_start(out=beta_all[:], in_=beta.partition_broadcast(P))
-        nc.scalar.dma_start(out=rstd_all[:], in_=rstd.partition_broadcast(P))
+        row_bf = consts.tile([P, 2 * O], BF16, name="row_bf")
+        row_f32 = consts.tile([P, O], F32, name="row_f32")
+        nc.vector.memset(row_bf[:], 0.0)
+        nc.vector.memset(row_f32[:], 0.0)
+        nc.scalar.dma_start(out=row_bf[0:1, 0:O], in_=gamma.unsqueeze(0))
+        nc.scalar.dma_start(out=row_bf[0:1, O : 2 * O], in_=beta.unsqueeze(0))
+        nc.scalar.dma_start(out=row_f32[0:1, :], in_=rstd.unsqueeze(0))
+        ones_bf = consts.tile([P, P], BF16, name="ones_bf")
+        ones_f32 = consts.tile([P, P], F32, name="ones_f32")
+        nc.vector.memset(ones_bf[:], 1.0)
+        nc.vector.memset(ones_f32[:], 1.0)
+        gamma_beta_all = banks.tile([P, 2 * O], F32, name="bank0")
+        rstd_all = banks.tile([P, O], F32, name="bank1")
+        nc.tensor.matmul(out=gamma_beta_all[:], lhsT=ones_bf[:], rhs=row_bf[:], start=True, stop=True)
+        nc.tensor.matmul(out=rstd_all[:], lhsT=ones_f32[:], rhs=row_f32[:], start=True, stop=True)
 
         ident = consts.tile([P, P], F32, name="ident")
         make_identity(nc, ident[:])
@@ -90,7 +99,7 @@ def tile_dggcn_sparse_assemble_pa_v_kernel(tc, z, A, x, gamma, beta, y_hat, rstd
             picked = consts.tile([P, GROUPS, CH], F32, name=name + "_picked")
             nc.vector.tensor_tensor(
                 out=picked[:],
-                in0=all_channels[:].rearrange("p (cg ol) -> p cg ol", ol=CH),
+                in0=all_channels.rearrange("p (cg ol) -> p cg ol", ol=CH),
                 in1=own_ch[:].unsqueeze(1).to_broadcast([P, GROUPS, CH]),
                 op=ALU.mult,
             )
@@ -98,9 +107,9 @@ def tile_dggcn_sparse_assemble_pa_v_kernel(tc, z, A, x, gamma, beta, y_hat, rstd
             nc.vector.tensor_reduce(out=own[:], in_=picked[:], axis=AX.X, op=ALU.add)
             return own
 
-        ga = own_value(gamma_all, "ga")
-        be = own_value(beta_all, "be")
-        rs = own_value(rstd_all, "rs")
+        ga = own_value(gamma_beta_all[:, 0:O], "ga")
+        be = own_value(gamma_beta_all[:, O : 2 * O], "be")
+        rs = own_value(rstd_all[:], "rs")
         neg_be = consts.tile([P, GROUPS], F32, name="neg_be")
         nc.vector.tensor_scalar_mul(out=neg_be[:], in0=be[:], scalar1=-1.0)
         rs_ga = consts.tile([P, GROUPS], F32, name="rs_ga")

@@ -27,7 +27,7 @@ Z_STEPS = 2 * PASSES
 
 PRE_BANKS = 6
 ON_VECTOR = (0, PASSES - 1)
-SHARED_FROM = 12
+SHARED_FROM = 11
 RAW_BUFS = 4
 GROUPED_BUFS = 5
 
@@ -274,7 +274,7 @@ def tile_dggcn_sparse_assemble_pa_v_kernel(tc, z, A, x, gamma, beta, y_hat, rstd
         load_inputs(1)
         load_z_up_to(0)
         before_relu(0)
-        acc, totals = {}, None
+        acc, totals = {}, {}
         for c in range(PASSES):
             halves = 2 * (c + 2) + min(max(0, c - 2), 4)
             if c + 2 < PASSES:
@@ -287,11 +287,13 @@ def tile_dggcn_sparse_assemble_pa_v_kernel(tc, z, A, x, gamma, beta, y_hat, rstd
             if c + 1 in ON_VECTOR:
                 before_relu(c + 1)
             if c % 2 == 0:
-                totals = bank(PRE_BANKS + (c // 2) % 2, [P, CHUNKS, 2])
-            add_up(c, totals)
+                totals[c // 2] = bank(PRE_BANKS + (c // 2) % 2, [P, CHUNKS, 2])
+            add_up(c, totals[c // 2])
             if c >= 1:
                 quantise_z(c - 1)
             regroup_up_to(2 * (c + 2))
+            if c >= 2 and c % 2 == 0:
+                coefficients(c // 2 - 1, totals[c // 2 - 1])
             if c >= 2:
                 centre(c - 2)
                 finish(c - 2)
@@ -299,14 +301,13 @@ def tile_dggcn_sparse_assemble_pa_v_kernel(tc, z, A, x, gamma, beta, y_hat, rstd
                 regroup_up_to(halves)
             if c >= 3:
                 quantise_dy(c - 3)
-            if c % 2 == 1:
-                coefficients(c // 2, totals)
             if c == PASSES - 2:
                 for i in range(TILES - 1):
                     acc[i] = bank(i, [P, V])
                 for done in range(c - 2):
                     multiply(acc, done, range(TILES - 1))
             if c == PASSES - 1:
+                coefficients(GROUPS - 1, totals[GROUPS - 1])
                 acc[TILES - 1] = bank(TILES - 1, [P, V])
                 for done in range(c - 3):
                     multiply(acc, done, [TILES - 1])
@@ -344,10 +345,9 @@ def tile_dggcn_sparse_assemble_pa_v_kernel(tc, z, A, x, gamma, beta, y_hat, rstd
                     store(0, i)
                 stored = True
             quantise_z(zi)
-            if zi < Z_STEPS - 2:
+            if zi < Z_STEPS - 1:
                 multiply(acc, zi - PASSES, range(TILES))
         for i in range(TILES):
-            multiply(acc, PASSES - 2, [i])
             multiply(acc, PASSES - 1, [i])
             empty(acc, i)
             store(1, i)

@@ -213,7 +213,9 @@ def tile_dggcn_sparse_assemble_pa_v_kernel(tc, z, A, x, gamma, beta, y_hat, rstd
 
         def coefficients(cg, totals):
             nc.vector.tensor_reduce(out=coef[:, cg, :], in_=totals[:].rearrange("p k s -> p s k"), axis=AX.X, op=ALU.add)
-            nc.vector.tensor_mul(out=shift[:, cg : cg + 1], in0=coef[:, cg, 0:1], in1=rs_ga[:, cg : cg + 1])
+            nc.scalar.activation(
+                out=shift[:, cg : cg + 1], in_=coef[:, cg, 0:1], func=ACT.Copy, scale=rs_ga[:, cg : cg + 1]
+            )
 
         def centre(c):
             nc.vector.scalar_tensor_tensor(
@@ -283,22 +285,26 @@ def tile_dggcn_sparse_assemble_pa_v_kernel(tc, z, A, x, gamma, beta, y_hat, rstd
             masked_gradient(c)
             if c + 1 < PASSES and c + 1 not in ON_VECTOR:
                 before_relu_on_tensor(c + 1)
+            if c >= 2 and c % 2 == 0:
+                coefficients(c // 2 - 1, totals[c // 2 - 1])
+            if c >= 3:
+                quantise_z(c - 1)
             sum_with_y_hat(c)
             if c + 1 in ON_VECTOR:
                 before_relu(c + 1)
             if c % 2 == 0:
                 totals[c // 2] = bank(PRE_BANKS + (c // 2) % 2, [P, CHUNKS, 2])
             add_up(c, totals[c // 2])
-            if c >= 1:
+            if 1 <= c < 3:
                 quantise_z(c - 1)
             regroup_up_to(2 * (c + 2))
-            if c >= 2 and c % 2 == 0:
-                coefficients(c // 2 - 1, totals[c // 2 - 1])
             if c >= 2:
                 centre(c - 2)
                 finish(c - 2)
             if c < PASSES - 1:
                 regroup_up_to(halves)
+            if c == PASSES - 1:
+                coefficients(GROUPS - 1, totals[GROUPS - 1])
             if c >= 3:
                 quantise_dy(c - 3)
             if c == PASSES - 2:
@@ -307,7 +313,6 @@ def tile_dggcn_sparse_assemble_pa_v_kernel(tc, z, A, x, gamma, beta, y_hat, rstd
                 for done in range(c - 2):
                     multiply(acc, done, range(TILES - 1))
             if c == PASSES - 1:
-                coefficients(GROUPS - 1, totals[GROUPS - 1])
                 acc[TILES - 1] = bank(TILES - 1, [P, V])
                 for done in range(c - 3):
                     multiply(acc, done, [TILES - 1])
@@ -338,7 +343,7 @@ def tile_dggcn_sparse_assemble_pa_v_kernel(tc, z, A, x, gamma, beta, y_hat, rstd
         multiply(acc, 1, range(TILES))
         stored = False
         for zi in range(PASSES + 2, Z_STEPS):
-            regroup_up_to(2 * (zi + 1))
+            regroup_up_to(2 * (zi + 2))
             load_z_up_to(Z_STEPS - 1)
             if state["loaded"] == Z_STEPS and not stored:
                 for i in range(TILES):

@@ -273,15 +273,16 @@ def tile_dggcn_sparse_assemble_pa_v_kernel(tc, z, A, x, gamma, beta, y_hat, rstd
                 state["halves"] += 1
 
         load_inputs(0)
-        load_inputs(1)
         load_z_up_to(0)
+        load_inputs(1)
+        load_z_up_to(1)
         before_relu(0)
         acc, totals = {}, {}
         for c in range(PASSES):
             halves = 2 * (c + 2) + min(max(0, c - 2), 4)
             if c + 2 < PASSES:
                 load_inputs(c + 2)
-            load_z_up_to((halves - 1) // 2 + min(c, 1))
+            load_z_up_to((halves - 1) // 2 + 1)
             masked_gradient(c)
             if c + 1 < PASSES and c + 1 not in ON_VECTOR:
                 before_relu_on_tensor(c + 1)

@@ -95,31 +95,30 @@ def tile_dggcn_sparse_assemble_pa_v_kernel(tc, z, A, x, gamma, beta, y_hat, rstd
             scalar1=-1.0 / COUNT,
         )
 
-        def own_value(all_channels, name):
-            picked = consts.tile([P, GROUPS, CH], F32, name=name + "_picked")
+        sums = consts.tile([P, PASSES, CHUNKS, 2], F32, name="sums")
+        nc.vector.memset(sums[:], 0.0)
+
+        every = {"ga": gamma_beta_all[:, 0:O], "be": gamma_beta_all[:, O : 2 * O], "rs": rstd_all[:]}
+        picked, own = {}, {}
+        for name in ("ga", "be", "rs"):
+            picked[name] = consts.tile([P, GROUPS, CH], F32, name=name + "_picked")
             nc.vector.tensor_tensor(
-                out=picked[:],
-                in0=all_channels.rearrange("p (cg ol) -> p cg ol", ol=CH),
+                out=picked[name][:],
+                in0=every[name].rearrange("p (cg ol) -> p cg ol", ol=CH),
                 in1=own_ch[:].unsqueeze(1).to_broadcast([P, GROUPS, CH]),
                 op=ALU.mult,
             )
-            own = consts.tile([P, GROUPS], F32, name=name)
-            nc.vector.tensor_reduce(out=own[:], in_=picked[:], axis=AX.X, op=ALU.add)
-            return own
-
-        ga = own_value(gamma_beta_all[:, 0:O], "ga")
-        be = own_value(gamma_beta_all[:, O : 2 * O], "be")
-        rs = own_value(rstd_all[:], "rs")
+        for name in ("ga", "be", "rs"):
+            own[name] = consts.tile([P, GROUPS], F32, name=name)
+            nc.vector.tensor_reduce(out=own[name][:], in_=picked[name][:], axis=AX.X, op=ALU.add)
+        ga, be, rs = own["ga"], own["be"], own["rs"]
         neg_be = consts.tile([P, GROUPS], F32, name="neg_be")
         nc.vector.tensor_scalar_mul(out=neg_be[:], in0=be[:], scalar1=-1.0)
         rs_ga = consts.tile([P, GROUPS], F32, name="rs_ga")
         nc.vector.tensor_mul(out=rs_ga[:], in0=rs[:], in1=ga[:])
         diag_ga = [consts.tile([P, P], F32, name="diag_ga%d" % cg) for cg in range(GROUPS)]
         for cg in range(GROUPS):
-            nc.vector.tensor_scalar_mul(out=diag_ga[cg][:], in0=ident[:], scalar1=ga[:, cg : cg + 1])
-
-        sums = consts.tile([P, PASSES, CHUNKS, 2], F32, name="sums")
-        nc.vector.memset(sums[:], 0.0)
+            nc.scalar.activation(out=diag_ga[cg][:], in_=ident[:], func=ACT.Copy, scale=ga[:, cg : cg + 1])
         coef = consts.tile([P, GROUPS, 2], F32, name="coef")
         shift = consts.tile([P, GROUPS], F32, name="shift")
 
@@ -279,7 +278,7 @@ def tile_dggcn_sparse_assemble_pa_v_kernel(tc, z, A, x, gamma, beta, y_hat, rstd
         before_relu(0)
         acc, totals = {}, {}
         for c in range(PASSES):
-            halves = 2 * (c + 2) + min(max(0, c - 2), 4)
+            halves = 2 * (c + 2) + min(max(0, c - 1), 5)
             if c + 2 < PASSES:
                 load_inputs(c + 2)
             load_z_up_to((halves - 1) // 2 + 1)

@@ -26,7 +26,13 @@ CHUNKS = ROW // BANK
 Z_STEPS = 2 * PASSES
 
 PRE_BANKS = 6
-ON_VECTOR = (0, PASSES - 1)
+ON_VECTOR = (0, 1, 2)
+FIRST_ON_T = 3
+EARLY = (0, 1, 6)
+BY_TILE = 2
+Z_FIRST_FROM = 3
+Z_BEFORE_LAST = 21
+RT = 24
 SHARED_FROM = 11
 RAW_BUFS = 4
 GROUPED_BUFS = 5
@@ -64,13 +70,31 @@ def tile_dggcn_sparse_assemble_pa_v_kernel(tc, z, A, x, gamma, beta, y_hat, rstd
     ) as inputs, tc.tile_pool(name="works", bufs=1) as works, tc.tile_pool(name="raws", bufs=RAW_BUFS) as raws, tc.tile_pool(
         name="groupeds", bufs=GROUPED_BUFS
     ) as groupeds, tc.tile_pool(name="dygs", bufs=2) as dygs, tc.psum_pool(name="banks", bufs=1) as banks:
+        yh, x_c, g_c, mg, work, pre, raw, grouped, dyg = {}, {}, {}, {}, {}, {}, {}, {}, {}
+
+        def pieces(c):
+            n = 2 if c == 0 else 1
+            return [slice(i * ROW // n, (i + 1) * ROW // n) for i in range(n)]
+
+        def load_inputs(c, i):
+            if i == 0:
+                yh[c] = yhs.tile([P, ROW], F32, name="yh")
+                x_c[c] = inputs.tile([P, ROW], BF16, name="x_c")
+            cols = pieces(c)[i]
+            load_pass(nc, yh[c][:, cols], yh_v[c // 2, c % 2, :, :, cols])
+            load_pass(nc, x_c[c][:, cols], x_v[c // 2, c % 2, :, :, cols])
+            if i == len(pieces(c)) - 1:
+                g_c[c] = inputs.tile([P, ROW], BF16, name="g_c")
+                load_pass(nc, g_c[c], g_v[c // 2, c % 2])
+
         row_bf = consts.tile([P, 2 * O], BF16, name="row_bf")
         row_f32 = consts.tile([P, O], F32, name="row_f32")
         nc.vector.memset(row_bf[:], 0.0)
         nc.vector.memset(row_f32[:], 0.0)
-        nc.scalar.dma_start(out=row_bf[0:1, 0:O], in_=gamma.unsqueeze(0))
-        nc.scalar.dma_start(out=row_bf[0:1, O : 2 * O], in_=beta.unsqueeze(0))
-        nc.scalar.dma_start(out=row_f32[0:1, :], in_=rstd.unsqueeze(0))
+        load_inputs(0, 0)
+        nc.sync.dma_start(out=row_bf[0:1, 0:O], in_=gamma.unsqueeze(0))
+        nc.sync.dma_start(out=row_bf[0:1, O : 2 * O], in_=beta.unsqueeze(0))
+        nc.sync.dma_start(out=row_f32[0:1, :], in_=rstd.unsqueeze(0))
         ones_bf = consts.tile([P, P], BF16, name="ones_bf")
         ones_f32 = consts.tile([P, P], F32, name="ones_f32")
         nc.vector.memset(ones_bf[:], 1.0)
@@ -127,18 +151,8 @@ def tile_dggcn_sparse_assemble_pa_v_kernel(tc, z, A, x, gamma, beta, y_hat, rstd
         dy_codes = [codes.tile([P, V], U32, name="dy_codes%d" % c, align_bytes=64) for c in range(PASSES)]
         dy_scales = [codes.tile([P, V], U8, name="dy_scales%d" % c, align_bytes=64) for c in range(PASSES)]
 
-        yh, x_c, g_c, mg, work, pre, raw, grouped, dyg = {}, {}, {}, {}, {}, {}, {}, {}, {}
-
         def bank(b, shape):
             return banks.tile(shape, F32, name="bank%d" % b)
-
-        def load_inputs(c):
-            yh[c] = yhs.tile([P, ROW], F32, name="yh")
-            load_pass(nc, yh[c], yh_v[c // 2, c % 2])
-            x_c[c] = inputs.tile([P, ROW], BF16, name="x_c")
-            load_pass(nc, x_c[c], x_v[c // 2, c % 2])
-            g_c[c] = inputs.tile([P, ROW], BF16, name="g_c")
-            load_pass(nc, g_c[c], g_v[c // 2, c % 2])
 
         def load_z(zi):
             s_pair, c = divmod(zi, PASSES)
@@ -161,14 +175,20 @@ def tile_dggcn_sparse_assemble_pa_v_kernel(tc, z, A, x, gamma, beta, y_hat, rstd
 
         def before_relu(c):
             work[c] = works.tile([P, ROW], F32, name="work")
-            nc.vector.scalar_tensor_tensor(
-                out=work[c][:], in0=yh[c][:], scalar=ga[:, c // 2 : c // 2 + 1], in1=x_c[c][:], op0=ALU.mult, op1=ALU.add
-            )
+            for cols in pieces(c):
+                nc.vector.scalar_tensor_tensor(
+                    out=work[c][:, cols],
+                    in0=yh[c][:, cols],
+                    scalar=ga[:, c // 2 : c // 2 + 1],
+                    in1=x_c[c][:, cols],
+                    op0=ALU.mult,
+                    op1=ALU.add,
+                )
 
         def before_relu_on_tensor(c):
             for k in range(CHUNKS):
                 cols = slice(k * BANK, (k + 1) * BANK)
-                pre[c, k] = bank((CHUNKS * (c - 1) + k) % PRE_BANKS, [P, BANK])
+                pre[c, k] = bank((CHUNKS * (c - FIRST_ON_T) + k) % PRE_BANKS, [P, BANK])
                 nc.tensor.matmul(out=pre[c, k][:], lhsT=diag_ga[c // 2][:], rhs=yh[c][:, cols], start=True, stop=False)
                 nc.tensor.matmul(out=pre[c, k][:], lhsT=ident_bf[:], rhs=x_c[c][:, cols], start=False, stop=True)
 
@@ -212,6 +232,8 @@ def tile_dggcn_sparse_assemble_pa_v_kernel(tc, z, A, x, gamma, beta, y_hat, rstd
 
         def coefficients(cg, totals):
             nc.vector.tensor_reduce(out=coef[:, cg, :], in_=totals[:].rearrange("p k s -> p s k"), axis=AX.X, op=ALU.add)
+
+        def make_shift(cg):
             nc.scalar.activation(
                 out=shift[:, cg : cg + 1], in_=coef[:, cg, 0:1], func=ACT.Copy, scale=rs_ga[:, cg : cg + 1]
             )
@@ -221,18 +243,36 @@ def tile_dggcn_sparse_assemble_pa_v_kernel(tc, z, A, x, gamma, beta, y_hat, rstd
                 out=yh[c][:], in0=yh[c][:], scalar=coef[:, c // 2, 1:2], in1=mg[c][:], op0=ALU.mult, op1=ALU.add
             )
 
-        def finish(c):
-            dyg[c] = dygs.tile([P, ROW], BF16, name="dy_grouped", align_bytes=64)
+        def half_cols(ap, half):
+            return ap.rearrange("p (t c) -> p t c", t=PACK)[:, :, half * V // 2 : (half + 1) * V // 2]
+
+        def centre_half(c, half, dst):
+            nc.vector.scalar_tensor_tensor(
+                out=dst[:, half * ROW // 2 : (half + 1) * ROW // 2].rearrange("p (t c) -> p t c", t=PACK),
+                in0=half_cols(yh[c][:], half),
+                scalar=coef[:, c // 2, 1:2],
+                in1=half_cols(mg[c][:], half),
+                op0=ALU.mult,
+                op1=ALU.add,
+            )
+
+        def finish_part(c, src, start, stop):
+            if start == 0:
+                dyg[c] = dygs.tile([P, ROW], BF16, name="dy_grouped", align_bytes=64)
             nc.scalar.activation(
-                out=grouped_view(dyg[c][:]),
-                in_=rows_view(yh[c][:]),
+                out=grouped_view(dyg[c][:, start * PACK : stop * PACK]),
+                in_=rows_view(src[:, start * PACK : stop * PACK]),
                 func=ACT.Identity,
                 scale=rs_ga[:, c // 2 : c // 2 + 1],
                 bias=shift[:, c // 2 : c // 2 + 1],
             )
 
-        def quantise_dy(c):
-            nc.vector.quantize_mx(out=dy_codes[c][:].bitcast(E5M2_X4), scales=dy_scales[c][:], in_=dyg[c][:])
+        def quantise_dy(c, start=0, stop=V):
+            nc.vector.quantize_mx(
+                out=dy_codes[c][:, start:stop].bitcast(E5M2_X4),
+                scales=dy_scales[c][:, start:stop],
+                in_=dyg[c][:, start * PACK : stop * PACK],
+            )
 
         def multiply(acc, c, tiles):
             for i in tiles:
@@ -271,25 +311,31 @@ def tile_dggcn_sparse_assemble_pa_v_kernel(tc, z, A, x, gamma, beta, y_hat, rstd
                 regroup_z(state["halves"])
                 state["halves"] += 1
 
-        load_inputs(0)
+        load_inputs(0, 1)
         load_z_up_to(0)
-        load_inputs(1)
+        load_inputs(1, 0)
         load_z_up_to(1)
         before_relu(0)
         acc, totals = {}, {}
         for c in range(PASSES):
-            halves = 2 * (c + 2) + min(max(0, c - 1), 5)
+            if c >= Z_FIRST_FROM:
+                load_z_up_to(Z_STEPS - 1)
             if c + 2 < PASSES:
-                load_inputs(c + 2)
-            load_z_up_to((halves - 1) // 2 + 1)
+                load_inputs(c + 2, 0)
+            load_z_up_to(c + 2)
+            last = c == PASSES - 1
             masked_gradient(c)
-            if c + 1 < PASSES and c + 1 not in ON_VECTOR:
+            if not last and c + 1 not in ON_VECTOR:
                 before_relu_on_tensor(c + 1)
             if c >= 2 and c % 2 == 0:
                 coefficients(c // 2 - 1, totals[c // 2 - 1])
             if c >= 3:
                 quantise_z(c - 1)
+            if c >= 2 and not last:
+                centre(c - 2)
             sum_with_y_hat(c)
+            if last:
+                centre(c - 2)
             if c + 1 in ON_VECTOR:
                 before_relu(c + 1)
             if c % 2 == 0:
@@ -297,46 +343,53 @@ def tile_dggcn_sparse_assemble_pa_v_kernel(tc, z, A, x, gamma, beta, y_hat, rstd
             add_up(c, totals[c // 2])
             if 1 <= c < 3:
                 quantise_z(c - 1)
-            regroup_up_to(2 * (c + 2))
+            regroup_up_to(2 * (c + 1) + max(0, c - 1) if not last else Z_BEFORE_LAST - 1)
             if c >= 2:
-                centre(c - 2)
-                finish(c - 2)
-            if c < PASSES - 1:
-                regroup_up_to(halves)
-            if c == PASSES - 1:
-                coefficients(GROUPS - 1, totals[GROUPS - 1])
+                if c % 2 == 0:
+                    make_shift(c // 2 - 1)
+                finish_part(c - 2, yh[c - 2], 0, V)
+            regroup_up_to(Z_BEFORE_LAST if last else 0)
             if c >= 3:
                 quantise_dy(c - 3)
             if c == PASSES - 2:
-                for i in range(TILES - 1):
+                for i in EARLY:
                     acc[i] = bank(i, [P, V])
                 for done in range(c - 2):
-                    multiply(acc, done, range(TILES - 1))
-            if c == PASSES - 1:
-                acc[TILES - 1] = bank(TILES - 1, [P, V])
-                for done in range(c - 3):
-                    multiply(acc, done, [TILES - 1])
-                multiply(acc, c - 3, range(TILES))
-
-        centre(PASSES - 2)
-        finish(PASSES - 2)
-        quantise_dy(PASSES - 3)
-        multiply(acc, PASSES - 3, range(TILES))
-        centre(PASSES - 1)
-        finish(PASSES - 1)
+                    multiply(acc, done, EARLY)
+        for i in range(TILES - 1):
+            if i not in EARLY:
+                acc[i] = bank(i, [P, V])
+        MID = tuple(i for i in range(TILES - 1) if i not in EARLY)
+        for done in range(PASSES - 4):
+            multiply(acc, done, MID)
+        multiply(acc, PASSES - 4, range(TILES - 1))
         quantise_z(PASSES - 1)
+        coefficients(GROUPS - 1, totals[GROUPS - 1])
+        make_shift(GROUPS - 1)
+        acc[TILES - 1] = bank(TILES - 1, [P, V])
+        for done in range(PASSES - 3):
+            multiply(acc, done, [TILES - 1])
+
+        for c in (PASSES - 2, PASSES - 1):
+            dst = work[PASSES - 1] if c == PASSES - 2 else yh[PASSES - 2]
+            for half in range(2):
+                centre_half(c, half, dst)
+                finish_part(c, dst, half * V // 2, (half + 1) * V // 2)
+            if c == PASSES - 2:
+                quantise_dy(PASSES - 3)
+                multiply(acc, PASSES - 3, range(TILES))
         quantise_dy(PASSES - 2)
         multiply(acc, PASSES - 2, range(TILES))
-        load_z_up_to(Z_STEPS - 1)
-        regroup_up_to(state["halves"] + 1)
-        quantise_z(PASSES)
-        quantise_dy(PASSES - 1)
+        for half in range(2):
+            quantise_dy(PASSES - 1, half * V // 2, (half + 1) * V // 2)
         multiply(acc, PASSES - 1, range(TILES))
-        quantise_z(PASSES + 1)
+        load_z_up_to(Z_STEPS - 1)
+        quantise_z(PASSES)
+        regroup_up_to(RT)
         for i in range(TILES):
             empty(acc, i)
-        regroup_up_to(2 * SHARED_FROM)
         load_z_up_to(Z_STEPS - 1)
+        quantise_z(PASSES + 1)
         for i in range(TILES):
             acc[i] = bank(i, [P, V])
         multiply(acc, 0, range(TILES))
@@ -350,9 +403,10 @@ def tile_dggcn_sparse_assemble_pa_v_kernel(tc, z, A, x, gamma, beta, y_hat, rstd
                     store(0, i)
                 stored = True
             quantise_z(zi)
-            if zi < Z_STEPS - 1:
+            if zi < Z_STEPS - BY_TILE:
                 multiply(acc, zi - PASSES, range(TILES))
         for i in range(TILES):
-            multiply(acc, PASSES - 1, [i])
+            for c in range(PASSES - BY_TILE, PASSES):
+                multiply(acc, c, [i])
             empty(acc, i)
             store(1, i)

@@ -42,8 +42,7 @@ BYTES = 2 * S * B * O * T * V + (2 + 2 + 4) * B * O * T * V + 4 * S * V * V + 8 
 
 
 def load_pass(nc, dst, src):
-    for bl in range(2):
-        nc.sync.dma_start(out=dst[bl:P:2], in_=src[bl])
+    nc.sync.dma_start(out=dst, in_=src)
 
 
 def grouped_view(ap):
@@ -57,11 +56,11 @@ def rows_view(ap):
 def tile_dggcn_sparse_assemble_pa_v_kernel(tc, z, A, x, gamma, beta, y_hat, rstd, grad_out, out):
     nc = tc.nc
 
-    rows = "(bh bl) (cg ol) (tq j) w -> cg bh bl (ol tq) (j w)"
+    rows = "(bh bl) (cg ol) (tq j) w -> cg bh (ol tq) bl (j w)"
     x_v = x.rearrange(rows, bl=2, ol=CH, j=PACK)
     g_v = grad_out.rearrange(rows, bl=2, ol=CH, j=PACK)
     yh_v = y_hat.rearrange(rows, bl=2, ol=CH, j=PACK)
-    z_v = z.rearrange("s (bh bl) (cg ol) (tq j) v -> cg bh bl (ol tq) s (j v)", bl=2, ol=CH, j=PACK)
+    z_v = z.rearrange("s (bh bl) (cg ol) (tq j) v -> cg bh s (ol tq) bl (j v)", bl=2, ol=CH, j=PACK)
 
     with tc.manual_schedule(), tc.tile_pool(name="consts", bufs=1) as consts, tc.tile_pool(
         name="codes", bufs=1
@@ -85,7 +84,7 @@ def tile_dggcn_sparse_assemble_pa_v_kernel(tc, z, A, x, gamma, beta, y_hat, rstd
             load_pass(nc, x_c[c][:, cols], x_v[c // 2, c % 2, :, :, cols])
             if i == len(pieces(c)) - 1:
                 g_c[c] = inputs.tile([P, ROW], BF16, name="g_c")
-                load_pass(nc, g_c[c], g_v[c // 2, c % 2])
+                load_pass(nc, g_c[c][:], g_v[c // 2, c % 2])
 
         row_bf = consts.tile([P, 2 * O], BF16, name="row_bf")
         row_f32 = consts.tile([P, O], F32, name="row_f32")
@@ -157,7 +156,8 @@ def tile_dggcn_sparse_assemble_pa_v_kernel(tc, z, A, x, gamma, beta, y_hat, rstd
         def load_z(zi):
             s_pair, c = divmod(zi, PASSES)
             raw[zi] = raws.tile([P, 2, ROW], BF16, name="z_raw")
-            load_pass(nc, raw[zi], z_v[c // 2, c % 2, :, :, 2 * s_pair : 2 * s_pair + 2, :])
+            for h in range(2):
+                load_pass(nc, raw[zi][:, h, :], z_v[c // 2, c % 2, 2 * s_pair + h])
 
         def regroup_z(half):
             zi, h = divmod(half, 2)

@@ -26,15 +26,10 @@ CHUNKS = ROW // BANK
 Z_STEPS = 2 * PASSES
 
 PRE_BANKS = 6
-ON_VECTOR = (0, 1, 2)
-FIRST_ON_T = 3
-EARLY = (0, 1, 6)
 BY_TILE = 2
 Z_FIRST_FROM = 3
-Z_BEFORE_LAST = 21
-RT = 24
-SHARED_FROM = 11
-RAW_BUFS = 4
+SHARED_FROM = 10
+RAW_BUFS = 3
 GROUPED_BUFS = 5
 
 FLOPS = 2 * (S * V) * V * (O * B * T)
@@ -64,7 +59,7 @@ def tile_dggcn_sparse_assemble_pa_v_kernel(tc, z, A, x, gamma, beta, y_hat, rstd
 
     with tc.manual_schedule(), tc.tile_pool(name="consts", bufs=1) as consts, tc.tile_pool(
         name="codes", bufs=1
-    ) as codes, tc.tile_pool(name="yhs", bufs=5) as yhs, tc.tile_pool(name="mgs", bufs=3) as mgs, tc.tile_pool(
+    ) as codes, tc.tile_pool(name="yhs", bufs=6) as yhs, tc.tile_pool(name="mgs", bufs=4) as mgs, tc.tile_pool(
         name="inputs", bufs=3
     ) as inputs, tc.tile_pool(name="works", bufs=1) as works, tc.tile_pool(name="raws", bufs=RAW_BUFS) as raws, tc.tile_pool(
         name="groupeds", bufs=GROUPED_BUFS
@@ -72,7 +67,7 @@ def tile_dggcn_sparse_assemble_pa_v_kernel(tc, z, A, x, gamma, beta, y_hat, rstd
         yh, x_c, g_c, mg, work, pre, raw, grouped, dyg = {}, {}, {}, {}, {}, {}, {}, {}, {}
 
         def pieces(c):
-            n = 2 if c == 0 else 1
+            n = 2 if c < 2 else 1
             return [slice(i * ROW // n, (i + 1) * ROW // n) for i in range(n)]
 
         def load_inputs(c, i):
@@ -81,6 +76,8 @@ def tile_dggcn_sparse_assemble_pa_v_kernel(tc, z, A, x, gamma, beta, y_hat, rstd
                 x_c[c] = inputs.tile([P, ROW], BF16, name="x_c")
             cols = pieces(c)[i]
             load_pass(nc, yh[c][:, cols], yh_v[c // 2, c % 2, :, :, cols])
+            if c == 0 and i == 0:
+                load_constants()
             load_pass(nc, x_c[c][:, cols], x_v[c // 2, c % 2, :, :, cols])
             if i == len(pieces(c)) - 1:
                 g_c[c] = inputs.tile([P, ROW], BF16, name="g_c")
@@ -90,10 +87,13 @@ def tile_dggcn_sparse_assemble_pa_v_kernel(tc, z, A, x, gamma, beta, y_hat, rstd
         row_f32 = consts.tile([P, O], F32, name="row_f32")
         nc.vector.memset(row_bf[:], 0.0)
         nc.vector.memset(row_f32[:], 0.0)
+
+        def load_constants():
+            nc.sync.dma_start(out=row_bf[0:1, 0:O], in_=gamma.unsqueeze(0))
+            nc.sync.dma_start(out=row_bf[0:1, O : 2 * O], in_=beta.unsqueeze(0))
+            nc.sync.dma_start(out=row_f32[0:1, :], in_=rstd.unsqueeze(0))
+
         load_inputs(0, 0)
-        nc.sync.dma_start(out=row_bf[0:1, 0:O], in_=gamma.unsqueeze(0))
-        nc.sync.dma_start(out=row_bf[0:1, O : 2 * O], in_=beta.unsqueeze(0))
-        nc.sync.dma_start(out=row_f32[0:1, :], in_=rstd.unsqueeze(0))
         ones_bf = consts.tile([P, P], BF16, name="ones_bf")
         ones_f32 = consts.tile([P, P], F32, name="ones_f32")
         nc.vector.memset(ones_bf[:], 1.0)
@@ -121,27 +121,6 @@ def tile_dggcn_sparse_assemble_pa_v_kernel(tc, z, A, x, gamma, beta, y_hat, rstd
         sums = consts.tile([P, PASSES, CHUNKS, 2], F32, name="sums")
         nc.vector.memset(sums[:], 0.0)
 
-        every = {"ga": gamma_beta_all[:, 0:O], "be": gamma_beta_all[:, O : 2 * O], "rs": rstd_all[:]}
-        picked, own = {}, {}
-        for name in ("ga", "be", "rs"):
-            picked[name] = consts.tile([P, GROUPS, CH], F32, name=name + "_picked")
-            nc.vector.tensor_tensor(
-                out=picked[name][:],
-                in0=every[name].rearrange("p (cg ol) -> p cg ol", ol=CH),
-                in1=own_ch[:].unsqueeze(1).to_broadcast([P, GROUPS, CH]),
-                op=ALU.mult,
-            )
-        for name in ("ga", "be", "rs"):
-            own[name] = consts.tile([P, GROUPS], F32, name=name)
-            nc.vector.tensor_reduce(out=own[name][:], in_=picked[name][:], axis=AX.X, op=ALU.add)
-        ga, be, rs = own["ga"], own["be"], own["rs"]
-        neg_be = consts.tile([P, GROUPS], F32, name="neg_be")
-        nc.vector.tensor_scalar_mul(out=neg_be[:], in0=be[:], scalar1=-1.0)
-        rs_ga = consts.tile([P, GROUPS], F32, name="rs_ga")
-        nc.vector.tensor_mul(out=rs_ga[:], in0=rs[:], in1=ga[:])
-        diag_ga = [consts.tile([P, P], F32, name="diag_ga%d" % cg) for cg in range(GROUPS)]
-        for cg in range(GROUPS):
-            nc.scalar.activation(out=diag_ga[cg][:], in_=ident[:], func=ACT.Copy, scale=ga[:, cg : cg + 1])
         coef = consts.tile([P, GROUPS, 2], F32, name="coef")
         shift = consts.tile([P, GROUPS], F32, name="shift")
 
@@ -173,34 +152,42 @@ def tile_dggcn_sparse_assemble_pa_v_kernel(tc, z, A, x, gamma, beta, y_hat, rstd
                 in_=grouped[zi][:].rearrange("p h f -> p (h f)"),
             )
 
-        def before_relu(c):
-            work[c] = works.tile([P, ROW], F32, name="work")
-            for cols in pieces(c):
-                nc.vector.scalar_tensor_tensor(
-                    out=work[c][:, cols],
-                    in0=yh[c][:, cols],
-                    scalar=ga[:, c // 2 : c // 2 + 1],
-                    in1=x_c[c][:, cols],
-                    op0=ALU.mult,
-                    op1=ALU.add,
-                )
+        def on_vector(c):
+            return ROW if c == 0 else ROW // 2 if c <= 2 else 0
+
+        def before_relu(c, start, stop):
+            if start == 0:
+                work[c] = works.tile([P, ROW], F32, name="work")
+            nc.vector.scalar_tensor_tensor(
+                out=work[c][:, start:stop],
+                in0=yh[c][:, start:stop],
+                scalar=ga[:, c // 2 : c // 2 + 1],
+                in1=x_c[c][:, start:stop],
+                op0=ALU.mult,
+                op1=ALU.add,
+            )
+
+        def next_bank():
+            state["bank"] += 1
+            return bank((state["bank"] - 1) % PRE_BANKS, [P, BANK])
 
         def before_relu_on_tensor(c):
-            for k in range(CHUNKS):
+            for k in range(on_vector(c) // BANK, CHUNKS):
                 cols = slice(k * BANK, (k + 1) * BANK)
-                pre[c, k] = bank((CHUNKS * (c - FIRST_ON_T) + k) % PRE_BANKS, [P, BANK])
+                pre[c, k] = next_bank()
                 nc.tensor.matmul(out=pre[c, k][:], lhsT=diag_ga[c // 2][:], rhs=yh[c][:, cols], start=True, stop=False)
                 nc.tensor.matmul(out=pre[c, k][:], lhsT=ident_bf[:], rhs=x_c[c][:, cols], start=False, stop=True)
 
         def masked_gradient(c):
             mg[c] = mgs.tile([P, ROW], BF16, name="mg")
-            pieces = [(0, slice(0, ROW), work[c])] if c in ON_VECTOR else [
-                (k, slice(k * BANK, (k + 1) * BANK), pre[c, k]) for k in range(CHUNKS)
-            ]
-            for k, cols, before in pieces:
+            split = on_vector(c)
+            parts = [(slice(0, split), work[c][:, 0:split])] if split else []
+            for k in range(split // BANK, CHUNKS):
+                parts.append((slice(k * BANK, (k + 1) * BANK), pre[c, k][:]))
+            for k, (cols, before) in enumerate(parts):
                 nc.vector.scalar_tensor_tensor(
                     out=mg[c][:, cols],
-                    in0=before[:],
+                    in0=before,
                     scalar=neg_be[:, c // 2 : c // 2 + 1],
                     in1=g_c[c][:, cols],
                     op0=ALU.is_gt,
@@ -209,10 +196,8 @@ def tile_dggcn_sparse_assemble_pa_v_kernel(tc, z, A, x, gamma, beta, y_hat, rstd
                 )
 
         def sum_with_y_hat(c):
-            if c not in ON_VECTOR:
-                work[c] = works.tile([P, ROW], F32, name="work")
             nc.vector.scalar_tensor_tensor(
-                out=work[c][:],
+                out=g_c[c][:],
                 in0=mg[c][:],
                 scalar=1.0,
                 in1=yh[c][:],
@@ -299,7 +284,7 @@ def tile_dggcn_sparse_assemble_pa_v_kernel(tc, z, A, x, gamma, beta, y_hat, rstd
             s, vt = 2 * s_pair + i * P // V, i % (V // P)
             nc.sync.dma_start(out=out[s, vt * P : (vt + 1) * P, :], in_=result[i][:])
 
-        state = {"loaded": 0, "halves": 0}
+        state = {"loaded": 0, "halves": 0, "bank": 0}
 
         def load_z_up_to(last):
             while state["loaded"] <= min(last, Z_STEPS - 1, state["halves"] // 2 + RAW_BUFS - 1):
@@ -311,81 +296,135 @@ def tile_dggcn_sparse_assemble_pa_v_kernel(tc, z, A, x, gamma, beta, y_hat, rstd
                 regroup_z(state["halves"])
                 state["halves"] += 1
 
+        def branches(c):
+            return 2 * (c + 1) + max(0, c - 1)
+
         load_inputs(0, 1)
         load_z_up_to(0)
         load_inputs(1, 0)
+        load_inputs(1, 1)
         load_z_up_to(1)
-        before_relu(0)
+
+        every = {"ga": gamma_beta_all[:, 0:O], "be": gamma_beta_all[:, O : 2 * O], "rs": rstd_all[:]}
+        picked, own = {}, {}
+
+        def pick(name):
+            picked[name] = consts.tile([P, GROUPS, CH], F32, name=name + "_picked")
+            nc.vector.tensor_tensor(
+                out=picked[name][:],
+                in0=every[name].rearrange("p (cg ol) -> p cg ol", ol=CH),
+                in1=own_ch[:].unsqueeze(1).to_broadcast([P, GROUPS, CH]),
+                op=ALU.mult,
+            )
+
+        def add_picked(name):
+            own[name] = consts.tile([P, GROUPS], F32, name=name)
+            nc.vector.tensor_reduce(out=own[name][:], in_=picked[name][:], axis=AX.X, op=ALU.add)
+            return own[name]
+
+        pick("ga")
+        pick("be")
+        ga = add_picked("ga")
+        be = add_picked("be")
+        before_relu(0, 0, ROW // 2)
+        neg_be = consts.tile([P, GROUPS], F32, name="neg_be")
+        nc.vector.tensor_scalar_mul(out=neg_be[:], in0=be[:], scalar1=-1.0)
+        before_relu(0, ROW // 2, ROW)
+        pick("rs")
+        rs = add_picked("rs")
+        diag_ga = [consts.tile([P, P], F32, name="diag_ga%d" % cg) for cg in range(GROUPS)]
+        for cg in range(GROUPS):
+            nc.scalar.activation(out=diag_ga[cg][:], in_=ident[:], func=ACT.Copy, scale=ga[:, cg : cg + 1])
+        rs_ga = consts.tile([P, GROUPS], F32, name="rs_ga")
         acc, totals = {}, {}
-        for c in range(PASSES):
+        A, C = PASSES - 2, PASSES - 1
+        for c in range(A):
             if c >= Z_FIRST_FROM:
                 load_z_up_to(Z_STEPS - 1)
-            if c + 2 < PASSES:
-                load_inputs(c + 2, 0)
+            load_inputs(c + 2, 0)
             load_z_up_to(c + 2)
-            last = c == PASSES - 1
             masked_gradient(c)
-            if not last and c + 1 not in ON_VECTOR:
-                before_relu_on_tensor(c + 1)
+            if c == 0:
+                nc.vector.tensor_mul(out=rs_ga[:], in0=rs[:], in1=ga[:])
             if c >= 2 and c % 2 == 0:
                 coefficients(c // 2 - 1, totals[c // 2 - 1])
-            if c >= 3:
+            before_relu_on_tensor(c + 1)
+            if c >= 1:
                 quantise_z(c - 1)
-            if c >= 2 and not last:
+            if c >= 2:
                 centre(c - 2)
+            if c > 0 and on_vector(c + 1):
+                before_relu(c + 1, 0, on_vector(c + 1))
             sum_with_y_hat(c)
-            if last:
-                centre(c - 2)
-            if c + 1 in ON_VECTOR:
-                before_relu(c + 1)
+            if c == 0:
+                before_relu(c + 1, 0, on_vector(c + 1))
             if c % 2 == 0:
                 totals[c // 2] = bank(PRE_BANKS + (c // 2) % 2, [P, CHUNKS, 2])
             add_up(c, totals[c // 2])
-            if 1 <= c < 3:
-                quantise_z(c - 1)
-            regroup_up_to(2 * (c + 1) + max(0, c - 1) if not last else Z_BEFORE_LAST - 1)
+            regroup_up_to(branches(c))
             if c >= 2:
                 if c % 2 == 0:
                     make_shift(c // 2 - 1)
                 finish_part(c - 2, yh[c - 2], 0, V)
-            regroup_up_to(Z_BEFORE_LAST if last else 0)
             if c >= 3:
                 quantise_dy(c - 3)
-            if c == PASSES - 2:
-                for i in EARLY:
-                    acc[i] = bank(i, [P, V])
-                for done in range(c - 2):
-                    multiply(acc, done, EARLY)
-        for i in range(TILES - 1):
-            if i not in EARLY:
-                acc[i] = bank(i, [P, V])
-        MID = tuple(i for i in range(TILES - 1) if i not in EARLY)
-        for done in range(PASSES - 4):
-            multiply(acc, done, MID)
-        multiply(acc, PASSES - 4, range(TILES - 1))
-        quantise_z(PASSES - 1)
+        load_z_up_to(Z_STEPS - 1)
+        masked_gradient(A)
+        before_relu_on_tensor(C)
+        coefficients(A // 2 - 1, totals[A // 2 - 1])
+        quantise_z(A - 1)
+        centre(A - 2)
+        regroup_up_to(branches(A))
+        make_shift(A // 2 - 1)
+        finish_part(A - 2, yh[A - 2], 0, V)
+        masked_gradient(C)
+        totals[A // 2] = bank(TILES - 1, [P, CHUNKS, 2])
+        OPEN = range(TILES - 1)
+        for i in OPEN:
+            acc[i] = bank(i, [P, V])
+        sum_with_y_hat(A)
+        multiply(acc, 0, OPEN)
+        multiply(acc, 1, OPEN)
+        add_up(A, totals[A // 2])
+        quantise_dy(A - 3)
+        multiply(acc, 2, OPEN)
+        sum_with_y_hat(C)
+        add_up(C, totals[A // 2])
+        multiply(acc, A - 3, OPEN)
+        load_z_up_to(Z_STEPS - 1)
+        centre(A - 1)
+        regroup_up_to(branches(A) + 1)
+        finish_part(A - 1, yh[A - 1], 0, V)
+        quantise_z(A)
         coefficients(GROUPS - 1, totals[GROUPS - 1])
         make_shift(GROUPS - 1)
+        quantise_dy(A - 2)
+        multiply(acc, A - 2, OPEN)
         acc[TILES - 1] = bank(TILES - 1, [P, V])
-        for done in range(PASSES - 3):
+        for done in range(A - 1):
             multiply(acc, done, [TILES - 1])
 
-        for c in (PASSES - 2, PASSES - 1):
-            dst = work[PASSES - 1] if c == PASSES - 2 else yh[PASSES - 2]
-            for half in range(2):
-                centre_half(c, half, dst)
-                finish_part(c, dst, half * V // 2, (half + 1) * V // 2)
-            if c == PASSES - 2:
-                quantise_dy(PASSES - 3)
-                multiply(acc, PASSES - 3, range(TILES))
-        quantise_dy(PASSES - 2)
-        multiply(acc, PASSES - 2, range(TILES))
-        for half in range(2):
-            quantise_dy(PASSES - 1, half * V // 2, (half + 1) * V // 2)
-        multiply(acc, PASSES - 1, range(TILES))
+        dst = {A: works.tile([P, ROW], F32, name="work"), C: yh[A]}
+
+        def last_dy(c, half):
+            centre_half(c, half, dst[c])
+            finish_part(c, dst[c], half * V // 2, (half + 1) * V // 2)
+
+        last_dy(A, 0)
+        last_dy(A, 1)
+        quantise_dy(A - 1)
+        multiply(acc, A - 1, range(TILES))
+        last_dy(C, 0)
+        quantise_dy(A)
+        multiply(acc, A, range(TILES))
+        last_dy(C, 1)
         load_z_up_to(Z_STEPS - 1)
+        quantise_dy(C, 0, V // 2)
+        quantise_z(C)
+        quantise_dy(C, V // 2, V)
+        multiply(acc, C, range(TILES))
         quantise_z(PASSES)
-        regroup_up_to(RT)
+        regroup_up_to(branches(A) + 3)
         for i in range(TILES):
             empty(acc, i)
         load_z_up_to(Z_STEPS - 1)

@@ -28,7 +28,7 @@ Z_STEPS = 2 * PASSES
 PRE_BANKS = 6
 BY_TILE = 2
 Z_FIRST_FROM = 3
-SHARED_FROM = 10
+SHARED_FROM = 12
 RAW_BUFS = 3
 GROUPED_BUFS = 5
 
@@ -123,6 +123,7 @@ def tile_dggcn_sparse_assemble_pa_v_kernel(tc, z, A, x, gamma, beta, y_hat, rstd
 
         coef = consts.tile([P, GROUPS, 2], F32, name="coef")
         shift = consts.tile([P, GROUPS], F32, name="shift")
+        factor = consts.tile([P, PASSES], F32, name="factor")
 
         z_codes = [codes.tile([P, 2 * V], U32, name="z_codes%d" % c, align_bytes=64) for c in range(PASSES)]
         z_scales = [codes.tile([P, 2 * V], U8, name="z_scales%d" % c, align_bytes=64) for c in range(PASSES)]
@@ -132,6 +133,11 @@ def tile_dggcn_sparse_assemble_pa_v_kernel(tc, z, A, x, gamma, beta, y_hat, rstd
         def bank(b, shape):
             return banks.tile(shape, F32, name="bank%d" % b)
 
+        def branches(c):
+            return (2, 4, 7)[c] if c < 3 else 10 + 7 * (c - 3) // 2
+
+        on_gpsimd = {c: branches(c - 1) for c in range(3, PASSES - 1)}
+
         def load_z(zi):
             s_pair, c = divmod(zi, PASSES)
             raw[zi] = raws.tile([P, 2, ROW], BF16, name="z_raw")
@@ -140,10 +146,27 @@ def tile_dggcn_sparse_assemble_pa_v_kernel(tc, z, A, x, gamma, beta, y_hat, rstd
 
         def regroup_z(half):
             zi, h = divmod(half, 2)
-            if h == 0:
+            if zi not in grouped:
                 grouped[zi] = groupeds.tile([P, 2, ROW], BF16, name="z_grouped", align_bytes=64)
             copy = nc.vector.tensor_copy if zi >= SHARED_FROM and h == 0 else nc.scalar.copy
-            copy(out=grouped_view(grouped[zi][:, h, :]), in_=rows_view(raw[zi][:, h, :]))
+            blocks = V // 8 if half in on_gpsimd.values() else V // 4
+            copy(
+                out=grouped_view(grouped[zi][:, h, :])[:, 0:blocks], in_=rows_view(raw[zi][:, h, :])[:, 0:blocks]
+            )
+
+        def regroup_on_gpsimd(c):
+            zi, h = divmod(on_gpsimd[c], 2)
+            if zi not in grouped:
+                grouped[zi] = groupeds.tile([P, 2, ROW], BF16, name="z_grouped", align_bytes=64)
+            nc.vector.memset(factor[:, c : c + 1], 1.0)
+            nc.gpsimd.tensor_scalar(
+                out=grouped[zi][:, h, ROW // 2 : ROW].rearrange("p (c t) -> p c t", t=PACK),
+                in0=raw[zi][:, h, :].rearrange("p (t c) -> p c t", t=PACK)[:, V // 2 : V],
+                scalar1=factor[:, c : c + 1],
+                scalar2=0.0,
+                op0=ALU.mult,
+                op1=ALU.add,
+            )
 
         def quantise_z(zi):
             nc.vector.quantize_mx(
@@ -179,6 +202,8 @@ def tile_dggcn_sparse_assemble_pa_v_kernel(tc, z, A, x, gamma, beta, y_hat, rstd
                 nc.tensor.matmul(out=pre[c, k][:], lhsT=ident_bf[:], rhs=x_c[c][:, cols], start=False, stop=True)
 
         def masked_gradient(c):
+            if c in on_gpsimd:
+                regroup_on_gpsimd(c)
             mg[c] = mgs.tile([P, ROW], BF16, name="mg")
             split = on_vector(c)
             parts = [(slice(0, split), work[c][:, 0:split])] if split else []
@@ -296,8 +321,6 @@ def tile_dggcn_sparse_assemble_pa_v_kernel(tc, z, A, x, gamma, beta, y_hat, rstd
                 regroup_z(state["halves"])
                 state["halves"] += 1
 
-        def branches(c):
-            return 2 * (c + 1) + max(0, c - 1)
 
         load_inputs(0, 1)
         load_z_up_to(0)
@@ -393,7 +416,7 @@ def tile_dggcn_sparse_assemble_pa_v_kernel(tc, z, A, x, gamma, beta, y_hat, rstd
         multiply(acc, A - 3, OPEN)
         load_z_up_to(Z_STEPS - 1)
         centre(A - 1)
-        regroup_up_to(branches(A) + 1)
+        regroup_up_to(branches(A) + 2)
         finish_part(A - 1, yh[A - 1], 0, V)
         quantise_z(A)
         coefficients(GROUPS - 1, totals[GROUPS - 1])

@@ -123,7 +123,6 @@ def tile_dggcn_sparse_assemble_pa_v_kernel(tc, z, A, x, gamma, beta, y_hat, rstd
 
         coef = consts.tile([P, GROUPS, 2], F32, name="coef")
         shift = consts.tile([P, GROUPS], F32, name="shift")
-        factor = consts.tile([P, PASSES], F32, name="factor")
 
         z_codes = [codes.tile([P, 2 * V], U32, name="z_codes%d" % c, align_bytes=64) for c in range(PASSES)]
         z_scales = [codes.tile([P, 2 * V], U8, name="z_scales%d" % c, align_bytes=64) for c in range(PASSES)]
@@ -158,11 +157,12 @@ def tile_dggcn_sparse_assemble_pa_v_kernel(tc, z, A, x, gamma, beta, y_hat, rstd
             zi, h = divmod(on_gpsimd[c], 2)
             if zi not in grouped:
                 grouped[zi] = groupeds.tile([P, 2, ROW], BF16, name="z_grouped", align_bytes=64)
-            nc.vector.memset(factor[:, c : c + 1], 1.0)
+            dst = grouped[zi][:, h, ROW // 2 : ROW]
+            nc.vector.memset(dst[:, 0:1], 0.0)
             nc.gpsimd.tensor_scalar(
-                out=grouped[zi][:, h, ROW // 2 : ROW].rearrange("p (c t) -> p c t", t=PACK),
+                out=dst.rearrange("p (c t) -> p c t", t=PACK),
                 in0=raw[zi][:, h, :].rearrange("p (t c) -> p c t", t=PACK)[:, V // 2 : V],
-                scalar1=factor[:, c : c + 1],
+                scalar1=1.0,
                 scalar2=0.0,
                 op0=ALU.mult,
                 op1=ALU.add,

@@ -28,7 +28,7 @@ Z_STEPS = 2 * PASSES
 PRE_BANKS = 6
 BY_TILE = 2
 Z_FIRST_FROM = 3
-SHARED_FROM = 12
+SHARED_FROM = 11
 RAW_BUFS = 3
 GROUPED_BUFS = 5
 
@@ -133,7 +133,7 @@ def tile_dggcn_sparse_assemble_pa_v_kernel(tc, z, A, x, gamma, beta, y_hat, rstd
             return banks.tile(shape, F32, name="bank%d" % b)
 
         def branches(c):
-            return (2, 4, 7)[c] if c < 3 else 10 + 7 * (c - 3) // 2
+            return 2 * (c + 1) + max(0, c - 1)
 
         on_gpsimd = {c: branches(c - 1) for c in range(3, PASSES - 1)}
 
@@ -447,7 +447,7 @@ def tile_dggcn_sparse_assemble_pa_v_kernel(tc, z, A, x, gamma, beta, y_hat, rstd
         quantise_dy(C, V // 2, V)
         multiply(acc, C, range(TILES))
         quantise_z(PASSES)
-        regroup_up_to(branches(A) + 3)
+        regroup_up_to(branches(A) + 4)
         for i in range(TILES):
             empty(acc, i)
         load_z_up_to(Z_STEPS - 1)

@@ -61,9 +61,11 @@ def tile_dggcn_sparse_assemble_pa_v_kernel(tc, z, A, x, gamma, beta, y_hat, rstd
         name="codes", bufs=1
     ) as codes, tc.tile_pool(name="yhs", bufs=6) as yhs, tc.tile_pool(name="mgs", bufs=4) as mgs, tc.tile_pool(
         name="inputs", bufs=3
-    ) as inputs, tc.tile_pool(name="works", bufs=1) as works, tc.tile_pool(name="raws", bufs=RAW_BUFS) as raws, tc.tile_pool(
-        name="groupeds", bufs=GROUPED_BUFS
-    ) as groupeds, tc.tile_pool(name="dygs", bufs=2) as dygs, tc.psum_pool(name="banks", bufs=1) as banks:
+    ) as inputs, tc.tile_pool(name="works", bufs=1) as works, tc.tile_pool(
+        name="raws", bufs=RAW_BUFS
+    ) as raws, tc.tile_pool(name="groupeds", bufs=GROUPED_BUFS) as groupeds, tc.tile_pool(
+        name="dygs", bufs=2
+    ) as dygs, tc.psum_pool(name="banks", bufs=1) as banks:
         yh, x_c, g_c, mg, work, pre, raw, grouped, dyg = {}, {}, {}, {}, {}, {}, {}, {}, {}
 
         def pieces(c):
@@ -176,7 +178,7 @@ def tile_dggcn_sparse_assemble_pa_v_kernel(tc, z, A, x, gamma, beta, y_hat, rstd
             )
 
         def on_vector(c):
-            return ROW if c == 0 else ROW // 2 if c <= 2 else 0
+            return ROW if c <= 1 else ROW // 2 if c == 2 else 0
 
         def before_relu(c, start, stop):
             if start == 0:
@@ -191,8 +193,8 @@ def tile_dggcn_sparse_assemble_pa_v_kernel(tc, z, A, x, gamma, beta, y_hat, rstd
             )
 
         def next_bank():
-            state["bank"] += 1
-            return bank((state["bank"] - 1) % PRE_BANKS, [P, BANK])
+            state["banks"] += 1
+            return bank((state["banks"] - 1) % PRE_BANKS, [P, BANK])
 
         def before_relu_on_tensor(c):
             for k in range(on_vector(c) // BANK, CHUNKS):
@@ -241,7 +243,9 @@ def tile_dggcn_sparse_assemble_pa_v_kernel(tc, z, A, x, gamma, beta, y_hat, rstd
             )
 
         def coefficients(cg, totals):
-            nc.vector.tensor_reduce(out=coef[:, cg, :], in_=totals[:].rearrange("p k s -> p s k"), axis=AX.X, op=ALU.add)
+            nc.vector.tensor_reduce(
+                out=coef[:, cg, :], in_=totals[:].rearrange("p k s -> p s k"), axis=AX.X, op=ALU.add
+            )
 
         def make_shift(cg):
             nc.scalar.activation(
@@ -309,7 +313,7 @@ def tile_dggcn_sparse_assemble_pa_v_kernel(tc, z, A, x, gamma, beta, y_hat, rstd
             s, vt = 2 * s_pair + i * P // V, i % (V // P)
             nc.sync.dma_start(out=out[s, vt * P : (vt + 1) * P, :], in_=result[i][:])
 
-        state = {"loaded": 0, "halves": 0, "bank": 0}
+        state = {"loaded": 0, "halves": 0, "banks": 0}
 
         def load_z_up_to(last):
             while state["loaded"] <= min(last, Z_STEPS - 1, state["halves"] // 2 + RAW_BUFS - 1):
@@ -360,8 +364,8 @@ def tile_dggcn_sparse_assemble_pa_v_kernel(tc, z, A, x, gamma, beta, y_hat, rstd
             nc.scalar.activation(out=diag_ga[cg][:], in_=ident[:], func=ACT.Copy, scale=ga[:, cg : cg + 1])
         rs_ga = consts.tile([P, GROUPS], F32, name="rs_ga")
         acc, totals = {}, {}
-        A, C = PASSES - 2, PASSES - 1
-        for c in range(A):
+        c6, c7 = PASSES - 2, PASSES - 1
+        for c in range(c6):
             if c >= Z_FIRST_FROM:
                 load_z_up_to(Z_STEPS - 1)
             load_inputs(c + 2, 0)
@@ -376,11 +380,11 @@ def tile_dggcn_sparse_assemble_pa_v_kernel(tc, z, A, x, gamma, beta, y_hat, rstd
                 quantise_z(c - 1)
             if c >= 2:
                 centre(c - 2)
-            if c > 0 and on_vector(c + 1):
+            if c >= 1 and on_vector(c + 1):
                 before_relu(c + 1, 0, on_vector(c + 1))
             sum_with_y_hat(c)
             if c == 0:
-                before_relu(c + 1, 0, on_vector(c + 1))
+                before_relu(1, 0, on_vector(1))
             if c % 2 == 0:
                 totals[c // 2] = bank(PRE_BANKS + (c // 2) % 2, [P, CHUNKS, 2])
             add_up(c, totals[c // 2])
@@ -391,63 +395,65 @@ def tile_dggcn_sparse_assemble_pa_v_kernel(tc, z, A, x, gamma, beta, y_hat, rstd
                 finish_part(c - 2, yh[c - 2], 0, V)
             if c >= 3:
                 quantise_dy(c - 3)
+
         load_z_up_to(Z_STEPS - 1)
-        masked_gradient(A)
-        before_relu_on_tensor(C)
-        coefficients(A // 2 - 1, totals[A // 2 - 1])
-        quantise_z(A - 1)
-        centre(A - 2)
-        regroup_up_to(branches(A))
-        make_shift(A // 2 - 1)
-        finish_part(A - 2, yh[A - 2], 0, V)
-        masked_gradient(C)
-        totals[A // 2] = bank(TILES - 1, [P, CHUNKS, 2])
-        OPEN = range(TILES - 1)
-        for i in OPEN:
+        masked_gradient(c6)
+        before_relu_on_tensor(c7)
+        coefficients(GROUPS - 2, totals[GROUPS - 2])
+        quantise_z(c6 - 1)
+        centre(c6 - 2)
+        regroup_up_to(branches(c6))
+        make_shift(GROUPS - 2)
+        finish_part(c6 - 2, yh[c6 - 2], 0, V)
+        masked_gradient(c7)
+        totals[GROUPS - 1] = bank(TILES - 1, [P, CHUNKS, 2])
+        free = range(TILES - 1)
+        for i in free:
             acc[i] = bank(i, [P, V])
-        sum_with_y_hat(A)
-        multiply(acc, 0, OPEN)
-        multiply(acc, 1, OPEN)
-        add_up(A, totals[A // 2])
-        quantise_dy(A - 3)
-        multiply(acc, 2, OPEN)
-        sum_with_y_hat(C)
-        add_up(C, totals[A // 2])
-        multiply(acc, A - 3, OPEN)
+        sum_with_y_hat(c6)
+        multiply(acc, 0, free)
+        multiply(acc, 1, free)
+        add_up(c6, totals[GROUPS - 1])
+        quantise_dy(c6 - 3)
+        multiply(acc, 2, free)
+        sum_with_y_hat(c7)
+        add_up(c7, totals[GROUPS - 1])
+        multiply(acc, c6 - 3, free)
         load_z_up_to(Z_STEPS - 1)
-        centre(A - 1)
-        regroup_up_to(branches(A) + 2)
-        finish_part(A - 1, yh[A - 1], 0, V)
-        quantise_z(A)
+        centre(c6 - 1)
+        regroup_up_to(branches(c6) + 2)
+        finish_part(c6 - 1, yh[c6 - 1], 0, V)
+        quantise_z(c6)
         coefficients(GROUPS - 1, totals[GROUPS - 1])
         make_shift(GROUPS - 1)
-        quantise_dy(A - 2)
-        multiply(acc, A - 2, OPEN)
+        quantise_dy(c6 - 2)
+        multiply(acc, c6 - 2, free)
         acc[TILES - 1] = bank(TILES - 1, [P, V])
-        for done in range(A - 1):
-            multiply(acc, done, [TILES - 1])
+        for c in range(c6 - 1):
+            multiply(acc, c, [TILES - 1])
 
-        dst = {A: works.tile([P, ROW], F32, name="work"), C: yh[A]}
+        centred = {c6: works.tile([P, ROW], F32, name="work"), c7: yh[c6]}
 
         def last_dy(c, half):
-            centre_half(c, half, dst[c])
-            finish_part(c, dst[c], half * V // 2, (half + 1) * V // 2)
+            centre_half(c, half, centred[c])
+            finish_part(c, centred[c], half * V // 2, (half + 1) * V // 2)
 
-        last_dy(A, 0)
-        last_dy(A, 1)
-        quantise_dy(A - 1)
-        multiply(acc, A - 1, range(TILES))
-        last_dy(C, 0)
-        quantise_dy(A)
-        multiply(acc, A, range(TILES))
-        last_dy(C, 1)
+        last_dy(c6, 0)
+        last_dy(c6, 1)
+        quantise_dy(c6 - 1)
+        multiply(acc, c6 - 1, range(TILES))
+        last_dy(c7, 0)
+        quantise_dy(c6)
+        multiply(acc, c6, range(TILES))
+        last_dy(c7, 1)
         load_z_up_to(Z_STEPS - 1)
-        quantise_dy(C, 0, V // 2)
-        quantise_z(C)
-        quantise_dy(C, V // 2, V)
-        multiply(acc, C, range(TILES))
+        quantise_dy(c7, 0, V // 2)
+        quantise_z(c7)
+        quantise_dy(c7, V // 2, V)
+        multiply(acc, c7, range(TILES))
+
         quantise_z(PASSES)
-        regroup_up_to(branches(A) + 4)
+        regroup_up_to(branches(c6) + 4)
         for i in range(TILES):
             empty(acc, i)
         load_z_up_to(Z_STEPS - 1)

import concourse.mybir as mybir
from concourse.masks import make_identity

F32 = mybir.dt.float32
BF16 = mybir.dt.bfloat16
U32 = mybir.dt.uint32
U8 = mybir.dt.uint8
E4M3_X4 = mybir.dt.float8_e4m3fn_x4
E5M2_X4 = mybir.dt.float8_e5m2_x4
ALU = mybir.AluOpType
ACT = mybir.ActivationFunctionType
AX = mybir.AxisListType

S, B, O, T, V = 4, 4, 64, 16, 512
P = 128
PACK = 4
PASSES = (O * B * T) // (P * PACK)
ROWS_PER_CH = 8
CH = P // ROWS_PER_CH
GROUPS = O // CH
ROW = PACK * V
TILES = 2 * V // P
COUNT = B * T * V
BANK = 512
CHUNKS = ROW // BANK
Z_STEPS = 2 * PASSES

PRE_BANKS = 6
BY_TILE = 2
Z_FIRST_FROM = 3
SHARED_FROM = 11
RAW_BUFS = 3
GROUPED_BUFS = 5

FLOPS = 2 * (S * V) * V * (O * B * T)
BYTES = 2 * S * B * O * T * V + (2 + 2 + 4) * B * O * T * V + 4 * S * V * V + 8 * O


def load_pass(nc, dst, src):
    nc.sync.dma_start(out=dst, in_=src)


def grouped_view(ap):
    return ap.rearrange("p (c i t) -> p c t i", i=4, t=PACK)


def rows_view(ap):
    return ap.rearrange("p (t c i) -> p c t i", i=4, t=PACK)


def tile_dggcn_sparse_assemble_pa_v_kernel(tc, z, A, x, gamma, beta, y_hat, rstd, grad_out, out):
    nc = tc.nc

    rows = "(bh bl) (cg ol) (tq j) w -> cg bh (ol tq) bl (j w)"
    x_v = x.rearrange(rows, bl=2, ol=CH, j=PACK)
    g_v = grad_out.rearrange(rows, bl=2, ol=CH, j=PACK)
    yh_v = y_hat.rearrange(rows, bl=2, ol=CH, j=PACK)
    z_v = z.rearrange("s (bh bl) (cg ol) (tq j) v -> cg bh s (ol tq) bl (j v)", bl=2, ol=CH, j=PACK)

    with tc.manual_schedule(), tc.tile_pool(name="consts", bufs=1) as consts, tc.tile_pool(
        name="codes", bufs=1
    ) as codes, tc.tile_pool(name="yhs", bufs=6) as yhs, tc.tile_pool(name="mgs", bufs=4) as mgs, tc.tile_pool(
        name="inputs", bufs=3
    ) as inputs, tc.tile_pool(name="works", bufs=1) as works, tc.tile_pool(
        name="raws", bufs=RAW_BUFS
    ) as raws, tc.tile_pool(name="groupeds", bufs=GROUPED_BUFS) as groupeds, tc.tile_pool(
        name="dygs", bufs=2
    ) as dygs, tc.psum_pool(name="banks", bufs=1) as banks:
        yh, x_c, g_c, mg, work, pre, raw, grouped, dyg = {}, {}, {}, {}, {}, {}, {}, {}, {}

        def pieces(c):
            n = 2 if c < 2 else 1
            return [slice(i * ROW // n, (i + 1) * ROW // n) for i in range(n)]

        def load_inputs(c, i):
            if i == 0:
                yh[c] = yhs.tile([P, ROW], F32, name="yh")
                x_c[c] = inputs.tile([P, ROW], BF16, name="x_c")
            cols = pieces(c)[i]
            load_pass(nc, yh[c][:, cols], yh_v[c // 2, c % 2, :, :, cols])
            if c == 0 and i == 0:
                load_constants()
            load_pass(nc, x_c[c][:, cols], x_v[c // 2, c % 2, :, :, cols])
            if i == len(pieces(c)) - 1:
                g_c[c] = inputs.tile([P, ROW], BF16, name="g_c")
                load_pass(nc, g_c[c][:], g_v[c // 2, c % 2])

        row_bf = consts.tile([P, 2 * O], BF16, name="row_bf")
        row_f32 = consts.tile([P, O], F32, name="row_f32")
        nc.vector.memset(row_bf[:], 0.0)
        nc.vector.memset(row_f32[:], 0.0)

        def load_constants():
            nc.sync.dma_start(out=row_bf[0:1, 0:O], in_=gamma.unsqueeze(0))
            nc.sync.dma_start(out=row_bf[0:1, O : 2 * O], in_=beta.unsqueeze(0))
            nc.sync.dma_start(out=row_f32[0:1, :], in_=rstd.unsqueeze(0))

        load_inputs(0, 0)
        ones_bf = consts.tile([P, P], BF16, name="ones_bf")
        ones_f32 = consts.tile([P, P], F32, name="ones_f32")
        nc.vector.memset(ones_bf[:], 1.0)
        nc.vector.memset(ones_f32[:], 1.0)
        gamma_beta_all = banks.tile([P, 2 * O], F32, name="bank0")
        rstd_all = banks.tile([P, O], F32, name="bank1")
        nc.tensor.matmul(out=gamma_beta_all[:], lhsT=ones_bf[:], rhs=row_bf[:], start=True, stop=True)
        nc.tensor.matmul(out=rstd_all[:], lhsT=ones_f32[:], rhs=row_f32[:], start=True, stop=True)

        ident = consts.tile([P, P], F32, name="ident")
        make_identity(nc, ident[:])
        ident_bf = consts.tile([P, P], BF16, name="ident_bf")
        nc.vector.tensor_copy(out=ident_bf[:], in_=ident[:])
        own_ch = consts.tile([P, CH], F32, name="own_ch")
        nc.vector.tensor_reduce(
            out=own_ch[:], in_=ident[:].rearrange("p (g i) -> p g i", i=ROWS_PER_CH), axis=AX.X, op=ALU.add
        )
        minus_mean = consts.tile([P, P], F32, name="minus_mean")
        nc.vector.tensor_scalar_mul(
            out=minus_mean[:].rearrange("p (g i) -> p g i", i=ROWS_PER_CH),
            in0=own_ch[:].unsqueeze(2).to_broadcast([P, CH, ROWS_PER_CH]),
            scalar1=-1.0 / COUNT,
        )

        sums = consts.tile([P, PASSES, CHUNKS, 2], F32, name="sums")
        nc.vector.memset(sums[:], 0.0)

        coef = consts.tile([P, GROUPS, 2], F32, name="coef")
        shift = consts.tile([P, GROUPS], F32, name="shift")

        z_codes = [codes.tile([P, 2 * V], U32, name="z_codes%d" % c, align_bytes=64) for c in range(PASSES)]
        z_scales = [codes.tile([P, 2 * V], U8, name="z_scales%d" % c, align_bytes=64) for c in range(PASSES)]
        dy_codes = [codes.tile([P, V], U32, name="dy_codes%d" % c, align_bytes=64) for c in range(PASSES)]
        dy_scales = [codes.tile([P, V], U8, name="dy_scales%d" % c, align_bytes=64) for c in range(PASSES)]

        def bank(b, shape):
            return banks.tile(shape, F32, name="bank%d" % b)

        def branches(c):
            return 2 * (c + 1) + max(0, c - 1)

        on_gpsimd = {c: branches(c - 1) for c in range(3, PASSES - 1)}

        def load_z(zi):
            s_pair, c = divmod(zi, PASSES)
            raw[zi] = raws.tile([P, 2, ROW], BF16, name="z_raw")
            for h in range(2):
                load_pass(nc, raw[zi][:, h, :], z_v[c // 2, c % 2, 2 * s_pair + h])

        def regroup_z(half):
            zi, h = divmod(half, 2)
            if zi not in grouped:
                grouped[zi] = groupeds.tile([P, 2, ROW], BF16, name="z_grouped", align_bytes=64)
            copy = nc.vector.tensor_copy if zi >= SHARED_FROM and h == 0 else nc.scalar.copy
            blocks = V // 8 if half in on_gpsimd.values() else V // 4
            copy(
                out=grouped_view(grouped[zi][:, h, :])[:, 0:blocks], in_=rows_view(raw[zi][:, h, :])[:, 0:blocks]
            )

        def regroup_on_gpsimd(c):
            zi, h = divmod(on_gpsimd[c], 2)
            if zi not in grouped:
                grouped[zi] = groupeds.tile([P, 2, ROW], BF16, name="z_grouped", align_bytes=64)
            dst = grouped[zi][:, h, ROW // 2 : ROW]
            nc.vector.memset(dst[:, 0:1], 0.0)
            nc.gpsimd.tensor_scalar(
                out=dst.rearrange("p (c t) -> p c t", t=PACK),
                in0=raw[zi][:, h, :].rearrange("p (t c) -> p c t", t=PACK)[:, V // 2 : V],
                scalar1=1.0,
                scalar2=0.0,
                op0=ALU.mult,
                op1=ALU.add,
            )

        def quantise_z(zi):
            nc.vector.quantize_mx(
                out=z_codes[zi % PASSES][:].bitcast(E4M3_X4),
                scales=z_scales[zi % PASSES][:],
                in_=grouped[zi][:].rearrange("p h f -> p (h f)"),
            )

        def on_vector(c):
            return ROW if c <= 1 else ROW // 2 if c == 2 else 0

        def before_relu(c, start, stop):
            if start == 0:
                work[c] = works.tile([P, ROW], F32, name="work")
            nc.vector.scalar_tensor_tensor(
                out=work[c][:, start:stop],
                in0=yh[c][:, start:stop],
                scalar=ga[:, c // 2 : c // 2 + 1],
                in1=x_c[c][:, start:stop],
                op0=ALU.mult,
                op1=ALU.add,
            )

        def next_bank():
            state["banks"] += 1
            return bank((state["banks"] - 1) % PRE_BANKS, [P, BANK])

        def before_relu_on_tensor(c):
            for k in range(on_vector(c) // BANK, CHUNKS):
                cols = slice(k * BANK, (k + 1) * BANK)
                pre[c, k] = next_bank()
                nc.tensor.matmul(out=pre[c, k][:], lhsT=diag_ga[c // 2][:], rhs=yh[c][:, cols], start=True, stop=False)
                nc.tensor.matmul(out=pre[c, k][:], lhsT=ident_bf[:], rhs=x_c[c][:, cols], start=False, stop=True)

        def masked_gradient(c):
            if c in on_gpsimd:
                regroup_on_gpsimd(c)
            mg[c] = mgs.tile([P, ROW], BF16, name="mg")
            split = on_vector(c)
            parts = [(slice(0, split), work[c][:, 0:split])] if split else []
            for k in range(split // BANK, CHUNKS):
                parts.append((slice(k * BANK, (k + 1) * BANK), pre[c, k][:]))
            for k, (cols, before) in enumerate(parts):
                nc.vector.scalar_tensor_tensor(
                    out=mg[c][:, cols],
                    in0=before,
                    scalar=neg_be[:, c // 2 : c // 2 + 1],
                    in1=g_c[c][:, cols],
                    op0=ALU.is_gt,
                    op1=ALU.mult,
                    accum_out=sums[:, c, k, 0:1],
                )

        def sum_with_y_hat(c):
            nc.vector.scalar_tensor_tensor(
                out=g_c[c][:],
                in0=mg[c][:],
                scalar=1.0,
                in1=yh[c][:],
                op0=ALU.mult,
                op1=ALU.mult,
                accum_out=sums[:, c, 0, 1:2],
            )

        def add_up(c, totals):
            nc.tensor.matmul(
                out=totals[:].rearrange("p k s -> p (k s)"),
                lhsT=minus_mean[:],
                rhs=sums[:, c, :, :].rearrange("p k s -> p (k s)"),
                start=(c % 2 == 0),
                stop=(c % 2 == 1),
            )

        def coefficients(cg, totals):
            nc.vector.tensor_reduce(
                out=coef[:, cg, :], in_=totals[:].rearrange("p k s -> p s k"), axis=AX.X, op=ALU.add
            )

        def make_shift(cg):
            nc.scalar.activation(
                out=shift[:, cg : cg + 1], in_=coef[:, cg, 0:1], func=ACT.Copy, scale=rs_ga[:, cg : cg + 1]
            )

        def centre(c):
            nc.vector.scalar_tensor_tensor(
                out=yh[c][:], in0=yh[c][:], scalar=coef[:, c // 2, 1:2], in1=mg[c][:], op0=ALU.mult, op1=ALU.add
            )

        def half_cols(ap, half):
            return ap.rearrange("p (t c) -> p t c", t=PACK)[:, :, half * V // 2 : (half + 1) * V // 2]

        def centre_half(c, half, dst):
            nc.vector.scalar_tensor_tensor(
                out=dst[:, half * ROW // 2 : (half + 1) * ROW // 2].rearrange("p (t c) -> p t c", t=PACK),
                in0=half_cols(yh[c][:], half),
                scalar=coef[:, c // 2, 1:2],
                in1=half_cols(mg[c][:], half),
                op0=ALU.mult,
                op1=ALU.add,
            )

        def finish_part(c, src, start, stop):
            if start == 0:
                dyg[c] = dygs.tile([P, ROW], BF16, name="dy_grouped", align_bytes=64)
            nc.scalar.activation(
                out=grouped_view(dyg[c][:, start * PACK : stop * PACK]),
                in_=rows_view(src[:, start * PACK : stop * PACK]),
                func=ACT.Identity,
                scale=rs_ga[:, c // 2 : c // 2 + 1],
                bias=shift[:, c // 2 : c // 2 + 1],
            )

        def quantise_dy(c, start=0, stop=V):
            nc.vector.quantize_mx(
                out=dy_codes[c][:, start:stop].bitcast(E5M2_X4),
                scales=dy_scales[c][:, start:stop],
                in_=dyg[c][:, start * PACK : stop * PACK],
            )

        def multiply(acc, c, tiles):
            for i in tiles:
                cols = slice(i * P, (i + 1) * P)
                nc.tensor.matmul_mx(
                    out=acc[i][:],
                    lhsT=z_codes[c][:, cols].bitcast(E4M3_X4),
                    lhsT_scale=z_scales[c][:, cols],
                    rhs=dy_codes[c][:].bitcast(E5M2_X4),
                    rhs_scale=dy_scales[c][:],
                    start=(c == 0),
                    stop=(c == PASSES - 1),
                )

        idle = [(inputs, "x_c"), (inputs, "g_c"), (mgs, "mg")]
        result = {}

        def empty(acc, i):
            pool, name = idle[i % len(idle)]
            result[i] = pool.tile([P, V], F32, name=name)
            (nc.vector.tensor_copy, nc.scalar.copy)[i % 2](out=result[i][:], in_=acc[i][:])

        def store(s_pair, i):
            s, vt = 2 * s_pair + i * P // V, i % (V // P)
            nc.sync.dma_start(out=out[s, vt * P : (vt + 1) * P, :], in_=result[i][:])

        state = {"loaded": 0, "halves": 0, "banks": 0}

        def load_z_up_to(last):
            while state["loaded"] <= min(last, Z_STEPS - 1, state["halves"] // 2 + RAW_BUFS - 1):
                load_z(state["loaded"])
                state["loaded"] += 1

        def regroup_up_to(halves):
            while state["halves"] < min(halves, 2 * state["loaded"]):
                regroup_z(state["halves"])
                state["halves"] += 1


        load_inputs(0, 1)
        load_z_up_to(0)
        load_inputs(1, 0)
        load_inputs(1, 1)
        load_z_up_to(1)

        every = {"ga": gamma_beta_all[:, 0:O], "be": gamma_beta_all[:, O : 2 * O], "rs": rstd_all[:]}
        picked, own = {}, {}

        def pick(name):
            picked[name] = consts.tile([P, GROUPS, CH], F32, name=name + "_picked")
            nc.vector.tensor_tensor(
                out=picked[name][:],
                in0=every[name].rearrange("p (cg ol) -> p cg ol", ol=CH),
                in1=own_ch[:].unsqueeze(1).to_broadcast([P, GROUPS, CH]),
                op=ALU.mult,
            )

        def add_picked(name):
            own[name] = consts.tile([P, GROUPS], F32, name=name)
            nc.vector.tensor_reduce(out=own[name][:], in_=picked[name][:], axis=AX.X, op=ALU.add)
            return own[name]

        pick("ga")
        pick("be")
        ga = add_picked("ga")
        be = add_picked("be")
        before_relu(0, 0, ROW // 2)
        neg_be = consts.tile([P, GROUPS], F32, name="neg_be")
        nc.vector.tensor_scalar_mul(out=neg_be[:], in0=be[:], scalar1=-1.0)
        before_relu(0, ROW // 2, ROW)
        pick("rs")
        rs = add_picked("rs")
        diag_ga = [consts.tile([P, P], F32, name="diag_ga%d" % cg) for cg in range(GROUPS)]
        for cg in range(GROUPS):
            nc.scalar.activation(out=diag_ga[cg][:], in_=ident[:], func=ACT.Copy, scale=ga[:, cg : cg + 1])
        rs_ga = consts.tile([P, GROUPS], F32, name="rs_ga")
        acc, totals = {}, {}
        c6, c7 = PASSES - 2, PASSES - 1
        for c in range(c6):
            if c >= Z_FIRST_FROM:
                load_z_up_to(Z_STEPS - 1)
            load_inputs(c + 2, 0)
            load_z_up_to(c + 2)
            masked_gradient(c)
            if c == 0:
                nc.vector.tensor_mul(out=rs_ga[:], in0=rs[:], in1=ga[:])
            if c >= 2 and c % 2 == 0:
                coefficients(c // 2 - 1, totals[c // 2 - 1])
            before_relu_on_tensor(c + 1)
            if c >= 1:
                quantise_z(c - 1)
            if c >= 2:
                centre(c - 2)
            if c >= 1 and on_vector(c + 1):
                before_relu(c + 1, 0, on_vector(c + 1))
            sum_with_y_hat(c)
            if c == 0:
                before_relu(1, 0, on_vector(1))
            if c % 2 == 0:
                totals[c // 2] = bank(PRE_BANKS + (c // 2) % 2, [P, CHUNKS, 2])
            add_up(c, totals[c // 2])
            regroup_up_to(branches(c))
            if c >= 2:
                if c % 2 == 0:
                    make_shift(c // 2 - 1)
                finish_part(c - 2, yh[c - 2], 0, V)
            if c >= 3:
                quantise_dy(c - 3)

        load_z_up_to(Z_STEPS - 1)
        masked_gradient(c6)
        before_relu_on_tensor(c7)
        coefficients(GROUPS - 2, totals[GROUPS - 2])
        quantise_z(c6 - 1)
        centre(c6 - 2)
        regroup_up_to(branches(c6))
        make_shift(GROUPS - 2)
        finish_part(c6 - 2, yh[c6 - 2], 0, V)
        masked_gradient(c7)
        totals[GROUPS - 1] = bank(TILES - 1, [P, CHUNKS, 2])
        free = range(TILES - 1)
        for i in free:
            acc[i] = bank(i, [P, V])
        sum_with_y_hat(c6)
        multiply(acc, 0, free)
        multiply(acc, 1, free)
        add_up(c6, totals[GROUPS - 1])
        quantise_dy(c6 - 3)
        multiply(acc, 2, free)
        sum_with_y_hat(c7)
        add_up(c7, totals[GROUPS - 1])
        multiply(acc, c6 - 3, free)
        load_z_up_to(Z_STEPS - 1)
        centre(c6 - 1)
        regroup_up_to(branches(c6) + 2)
        finish_part(c6 - 1, yh[c6 - 1], 0, V)
        quantise_z(c6)
        coefficients(GROUPS - 1, totals[GROUPS - 1])
        make_shift(GROUPS - 1)
        quantise_dy(c6 - 2)
        multiply(acc, c6 - 2, free)
        acc[TILES - 1] = bank(TILES - 1, [P, V])
        for c in range(c6 - 1):
            multiply(acc, c, [TILES - 1])

        centred = {c6: works.tile([P, ROW], F32, name="work"), c7: yh[c6]}

        def last_dy(c, half):
            centre_half(c, half, centred[c])
            finish_part(c, centred[c], half * V // 2, (half + 1) * V // 2)

        last_dy(c6, 0)
        last_dy(c6, 1)
        quantise_dy(c6 - 1)
        multiply(acc, c6 - 1, range(TILES))
        last_dy(c7, 0)
        quantise_dy(c6)
        multiply(acc, c6, range(TILES))
        last_dy(c7, 1)
        load_z_up_to(Z_STEPS - 1)
        quantise_dy(c7, 0, V // 2)
        quantise_z(c7)
        quantise_dy(c7, V // 2, V)
        multiply(acc, c7, range(TILES))

        quantise_z(PASSES)
        regroup_up_to(branches(c6) + 4)
        for i in range(TILES):
            empty(acc, i)
        load_z_up_to(Z_STEPS - 1)
        quantise_z(PASSES + 1)
        for i in range(TILES):
            acc[i] = bank(i, [P, V])
        multiply(acc, 0, range(TILES))
        multiply(acc, 1, range(TILES))
        stored = False
        for zi in range(PASSES + 2, Z_STEPS):
            regroup_up_to(2 * (zi + 2))
            load_z_up_to(Z_STEPS - 1)
            if state["loaded"] == Z_STEPS and not stored:
                for i in range(TILES):
                    store(0, i)
                stored = True
            quantise_z(zi)
            if zi < Z_STEPS - BY_TILE:
                multiply(acc, zi - PASSES, range(TILES))
        for i in range(TILES):
            for c in range(PASSES - BY_TILE, PASSES):
                multiply(acc, c, [i])
            empty(acc, i)
            store(1, i)
